import numpy as np
import ml_dtypes


def mxq(x, axis, fmt="e4m3"):
    dtype, down = {"e4m3": (ml_dtypes.float8_e4m3fn, 7), "e5m2": (ml_dtypes.float8_e5m2, 14)}[fmt]
    v = np.moveaxis(np.asarray(x, np.float32).astype(ml_dtypes.bfloat16).astype(np.float64), axis, -1)
    blocks = v.reshape(v.shape[:-1] + (-1, 32))
    amax = np.abs(blocks).max(-1, keepdims=True)
    byte = np.maximum(np.where(amax > 0, np.frexp(amax)[1] - 1 + 127, 0) - down, 1)
    scale = np.exp2(byte - 127.0)
    codes = (blocks / scale).astype(np.float32).astype(dtype).astype(np.float64)
    return np.moveaxis((codes * scale).reshape(v.shape), -1, axis)


WIDE = False


def mx_kscale(k):
    if not WIDE:
        return np.ones(k)
    levels = np.array([10, -10, 5, -5, 0])
    a = np.random.permutation(np.resize(levels, k // 512 * 4)).reshape(k // 512, 4)
    idx = np.arange(k)
    return np.exp2(a[idx // 512, idx % 128 // 32])


BF16 = ml_dtypes.bfloat16


def bf(x):
    return np.asarray(x, np.float32).astype(BF16)


def f64(x):
    return np.asarray(x).astype(np.float64)


B, HQ, HK, S, D, HID, BS = 1, 2, 1, 16384, 256, 512, 16
NB = S // BS
G = HQ // HK


def rotate_half(x):
    h = x.shape[-1] // 2
    return np.concatenate([-x[..., h:], x[..., :h]], axis=-1)


def pool_cat(x):
    b, h, s, d = x.shape
    xb = x.reshape(b, h, s // BS, BS, d)
    return np.concatenate([xb.mean(axis=3), xb.max(axis=3)], axis=-1)


def setup_inputs():
    s = mx_kscale(2 * D)[:D]
    s2 = np.concatenate([s, s])
    t = mx_kscale(HID)[:HID // 2]
    t2 = np.concatenate([t, t])
    q = bf(np.random.standard_normal((B, HQ, S, D)) * s)
    k = bf(np.random.standard_normal((B, HK, S, D)) * s)
    wq = bf(np.random.standard_normal((HQ, 2 * D, HID)) * 1.25 / np.sqrt(2 * D) / s2[:, None] * t2)
    wk = bf(np.random.standard_normal((HK, 2 * D, HID)) * 1.25 / np.sqrt(2 * D) / s2[:, None] / t2)
    keep = np.random.random((B, 1, NB, NB)) < 0.9
    mask = np.tril(np.ones((NB, NB), bool), 1) & (keep | np.eye(NB, dtype=bool) | np.eye(NB, k=1, dtype=bool))
    pos = np.arange(NB, dtype=np.float64)
    inv_freq = 1.0 / (10000.0 ** (np.arange(0, HID, 2, dtype=np.float64) / HID))
    freqs = pos[:, None] * inv_freq[None, :]
    emb = np.concatenate([freqs, freqs], axis=-1)
    cos = bf(np.broadcast_to(np.cos(emb)[None], (B, NB, HID)))
    sin = bf(np.broadcast_to(np.sin(emb)[None], (B, NB, HID)))
    return {"q": q, "k": k, "attention_mask": mask, "cos": cos, "sin": sin, "wq": wq, "wk": wk}


def reference(q, k, attention_mask, cos, sin, wq, wk):
    qh = mxq(pool_cat(f64(q)), 3, "e4m3") @ mxq(f64(wq), 1, "e4m3")
    kh = mxq(pool_cat(f64(k)), 3, "e4m3") @ mxq(f64(wk), 1, "e4m3")
    c, s = f64(cos)[:, None], f64(sin)[:, None]
    qh = qh * c + rotate_half(qh) * s
    kh = kh * c + rotate_half(kh) * s
    qg = qh.reshape(B, HK, G * NB, HID)
    attn = (mxq(qg, 3, "e4m3") @ mxq(kh.transpose(0, 1, 3, 2), 2, "e4m3")).reshape(B, HQ, NB, NB) / np.sqrt(HID)
    attn = np.where(attention_mask, attn, -1e9)
    e = np.exp(attn - attn.max(axis=-1, keepdims=True))
    return e / e.sum(axis=-1, keepdims=True)

@@ -1,0 +1,188 @@
+from contextlib import ExitStack
+import math
+
+import concourse.mybir as mybir
+from concourse.masks import make_identity
+
+BF16 = mybir.dt.bfloat16
+F32 = mybir.dt.float32
+I32 = mybir.dt.int32
+U32 = mybir.dt.uint32
+U8 = mybir.dt.uint8
+FP8X4 = mybir.dt.float8_e4m3fn_x4
+ALU = mybir.AluOpType
+ACT = mybir.ActivationFunctionType
+AX = mybir.AxisListType
+
+P = 128
+S_LEN = 16384
+D = 256
+HID = 512
+NB = 1024
+CHUNK = 2048
+NR = 8
+SCALE = 1.0 / math.sqrt(512.0)
+BIG = 2.0 ** 35
+
+FLOPS = 2 * 3 * NB * HID * HID + 2 * 2 * NB * NB * HID
+
+WIDE16 = ((1, 1), (1, 3), (1, 5), (1, 7))
+
+
+def tile_attngate_t_kernel(tc, q, k, attention_mask, cos, sin, wq, wk, out):
+    nc = tc.nc
+    with ExitStack() as ctx:
+        const = ctx.enter_context(tc.tile_pool(name="const", bufs=1))
+        xin = ctx.enter_context(tc.tile_pool(name="xin", bufs=4))
+        work = ctx.enter_context(tc.tile_pool(name="work", bufs=2))
+        soft = ctx.enter_context(tc.tile_pool(name="soft", bufs=2))
+        psum = ctx.enter_context(tc.psum_pool(name="psum", bufs=1))
+
+        ident = const.tile([P, P], BF16, name="ident")
+        make_identity(nc, ident[:])
+        perm8 = const.tile([P, P], BF16, name="perm8")
+        nc.vector.tensor_copy(
+            out=perm8[:].rearrange("p (h b) -> p h b", h=8),
+            in_=ident[:].rearrange("p (b h) -> p h b", h=8),
+        )
+        perm16 = const.tile([P, P], BF16, name="perm16")
+        nc.vector.tensor_copy(
+            out=perm16[:].rearrange("p (h b) -> p h b", h=16),
+            in_=ident[:].rearrange("p (b h) -> p h b", h=16),
+        )
+        cnt8 = const.tile([P, 16], F32, name="cnt8")
+        nc.vector.tensor_reduce(out=cnt8[:], in_=ident[:].rearrange("p (n h) -> p n h", h=8), axis=AX.X, op=ALU.add)
+        pool8 = const.tile([P, 16], BF16, name="pool8")
+        nc.vector.tensor_scalar(out=pool8[:], in0=cnt8[:], scalar1=1.0 / 16.0, scalar2=None, op0=ALU.mult)
+        cnt16 = const.tile([P, 8], F32, name="cnt16")
+        nc.vector.tensor_reduce(out=cnt16[:], in_=ident[:].rearrange("p (n h) -> p n h", h=16), axis=AX.X, op=ALU.add)
+        pool16 = const.tile([P, 8], BF16, name="pool16")
+        nc.vector.tensor_scalar(out=pool16[:], in0=cnt16[:], scalar1=1.0 / 16.0, scalar2=None, op0=ALU.mult)
+
+        def load_chunk(src, r, wide):
+            rows = src[r * CHUNK:(r + 1) * CHUNK, :]
+            x = xin.tile([P, 4096], BF16, name="x", tag="x")
+            if wide:
+                nc.sync.dma_start(out=x[:].rearrange("p (g d) -> p g d", g=16), in_=rows.rearrange("(g p) d -> p g d", g=16, p=P))
+            else:
+                nc.sync.dma_start(out=x[:].rearrange("p (g e) -> p g e", g=8), in_=rows.rearrange("(g p l) d -> p g (l d)", g=8, p=P, l=2))
+            return x
+
+        def load_weight(w, name):
+            raw = const.tile([P, 4, HID], BF16, name="raw_" + name)
+            nc.sync.dma_start(out=raw[:], in_=w.rearrange("(t p) n -> p t n", t=4, p=P))
+            grouped = const.tile([P, HID, 4], BF16, name="grp_" + name, align_bytes=64)
+            nc.vector.tensor_copy(out=grouped[:], in_=raw[:].rearrange("p t n -> p n t"))
+            codes = const.tile([P, HID], U32, name="wc_" + name, align_bytes=64)
+            scales = const.tile([P, HID], U8, name="ws_" + name, align_bytes=64)
+            nc.vector.quantize_mx(out=codes[:].bitcast(FP8X4), scales=scales[:], in_=grouped[:].rearrange("p n t -> p (n t)"))
+            return codes, scales
+
+        kc = const.tile([P, NB], U32, name="kc", align_bytes=64)
+        ks = const.tile([P, NB], U8, name="ks", align_bytes=64)
+
+        def pooled_rope(x, r, wide, wcodes, wscales, codes_out, scales_out):
+            groups = 16 if wide else 8
+            meanps = psum.tile([P, 2, P], F32, name="meanps", tag="mean")
+            first = work.tile([P, 2, groups, 64], BF16, name="first", tag="first%d" % groups)
+            if wide:
+                xv = x[:].rearrange("p (g d) -> p g d", g=16)
+                for g in range(16):
+                    for c in range(2):
+                        nc.tensor.matmul(out=meanps[:, c, g * 8:(g + 1) * 8], lhsT=xv[:, g, c * P:(c + 1) * P], rhs=pool16[:], start=True, stop=True)
+                src = xv
+                perm = perm16
+            else:
+                xv = x[:].rearrange("p (g e) -> p g e", g=8)
+                for g in range(8):
+                    for c in range(2):
+                        for l in range(2):
+                            nc.tensor.matmul(
+                                out=meanps[:, c, g * 16:(g + 1) * 16],
+                                lhsT=xv[:, g, l * D + c * P:l * D + (c + 1) * P],
+                                rhs=pool8[:], start=(l == 0), stop=(l == 1),
+                            )
+                l1 = work.tile([P, 8, D], BF16, name="l1", tag="l1")
+                nc.vector.tensor_tensor(out=l1[:], in0=xv[:, :, 0:D], in1=xv[:, :, D:2 * D], op=ALU.max)
+                src = l1
+                perm = perm8
+            for c in range(2):
+                for half in range(groups // 8):
+                    tp = psum.tile([P, 8, P], BF16, name="tp", tag="tp", bufs=3)
+                    for g in range(8):
+                        nc.tensor.transpose(out=tp[:, g, :], in_=src[:, half * 8 + g, c * P:(c + 1) * P], identity=perm[:])
+                    hi = work.tile([P, 8, 64], BF16, name="hi", tag="hi", bufs=3)
+                    nc.scalar.copy(out=hi[:], in_=tp[:, :, 64:128])
+                    nc.vector.tensor_tensor(out=first[:, c, half * 8:(half + 1) * 8, :], in0=tp[:, :, 0:64], in1=hi[:], op=ALU.max)
+            cur = first
+            width = 64
+            while width > P // groups:
+                width = width // 2
+                nxt = work.tile([P, 2, groups, width], BF16, name="lvl", tag="lvl%d_%d" % (groups, width))
+                nc.vector.tensor_tensor(out=nxt[:], in0=cur[:, :, :, 0:width], in1=cur[:, :, :, width:2 * width], op=ALU.max)
+                cur = nxt
+            grp = work.tile([P, P, 4], BF16, name="grp", tag="grp", align_bytes=64)
+            nc.scalar.copy(out=grp[:, :, 0:2], in_=meanps[:].rearrange("p c b -> p b c"))
+            nc.scalar.copy(out=grp[:, :, 2:4], in_=cur[:].rearrange("p c g b -> p (g b) c"))
+            pc = work.tile([P, P], U32, name="pc", tag="pc", align_bytes=64)
+            pscale = work.tile([P, P], U8, name="pscale", tag="pscale", align_bytes=64)
+            nc.vector.quantize_mx(out=pc[:].bitcast(FP8X4), scales=pscale[:], in_=grp[:].rearrange("p b t -> p (b t)"))
+            xps = psum.tile([P, HID], F32, name="xps", tag="xps")
+            nc.tensor.matmul_mx(out=xps[:], lhsT=pc[:].bitcast(FP8X4), lhsT_scale=pscale[:], rhs=wcodes[:].bitcast(FP8X4), rhs_scale=wscales[:], start=True, stop=True)
+            m1 = work.tile([P, HID], F32, name="m1", tag="m1")
+            nc.vector.tensor_tensor(out=m1[:], in0=xps[:], in1=cos_sb[:, r, :], op=ALU.mult)
+            m2 = work.tile([P, HID], F32, name="m2", tag="m2")
+            nc.vector.tensor_tensor(out=m2[:, 0:256], in0=xps[:, 256:512], in1=nsin_sb[:, r, :], op=ALU.mult)
+            nc.vector.tensor_tensor(out=m2[:, 256:512], in0=xps[:, 0:256], in1=sin_sb[:, r, 256:512], op=ALU.mult)
+            y = work.tile([P, HID], BF16, name="y", tag="y")
+            nc.vector.tensor_tensor(out=y[:], in0=m1[:], in1=m2[:], op=ALU.add)
+            yt = psum.tile([P, 4, P], BF16, name="yt", tag="yt")
+            for t in range(4):
+                nc.tensor.transpose(out=yt[:, t, :], in_=y[:, t * P:(t + 1) * P], identity=ident[:])
+            g2 = work.tile([P, P, 4], BF16, name="g2", tag="g2", align_bytes=64)
+            nc.scalar.copy(out=g2[:], in_=yt[:].rearrange("p t b -> p b t"))
+            nc.vector.quantize_mx(out=codes_out.bitcast(FP8X4), scales=scales_out, in_=g2[:].rearrange("p b t -> p (b t)"))
+
+        x0 = load_chunk(k[0, 0], 0, False)
+        wk_c, wk_s = load_weight(wk[0], "k")
+        cos_sb = const.tile([P, NR, HID], BF16, name="cos_sb")
+        nc.sync.dma_start(out=cos_sb[:], in_=cos[0].rearrange("(r p) h -> p r h", p=P))
+        sin_sb = const.tile([P, NR, HID], BF16, name="sin_sb")
+        nc.sync.dma_start(out=sin_sb[:], in_=sin[0].rearrange("(r p) h -> p r h", p=P))
+        nsin_sb = const.tile([P, NR, 256], BF16, name="nsin_sb")
+        nc.vector.tensor_scalar(out=nsin_sb[:], in0=sin_sb[:, :, 0:256], scalar1=-1.0, scalar2=None, op0=ALU.mult)
+        for r in range(NR):
+            x = x0 if r == 0 else load_chunk(k[0, 0], r, False)
+            pooled_rope(x, r, False, wk_c, wk_s, kc[:, r * P:(r + 1) * P], ks[:, r * P:(r + 1) * P])
+        wq_cs = [load_weight(wq[h], "q%d" % h) for h in range(2)]
+
+        mask32 = attention_mask[0, 0].bitcast(I32).rearrange("(r p) w -> r p w", p=P)
+        for r in range(NR):
+            mraw = soft.tile([P, 2 * NB], I32, name="mraw", tag="mraw")
+            nc.sync.dma_start(out=mraw[:], in_=mask32[r])
+            bias = soft.tile([P, NB], BF16, name="bias", tag="bias")
+            nc.scalar.activation(out=bias[:], in_=mraw[:].bitcast(U32).rearrange("p (w two) -> p w two", two=2)[:, :, 0], func=ACT.Copy, bias=-BIG, scale=BIG)
+            for h in range(2):
+                wide = (h, r) in WIDE16
+                x = load_chunk(q[0, h], r, wide)
+                qc = work.tile([P, P], U32, name="qc", tag="qc", align_bytes=64)
+                qs = work.tile([P, P], U8, name="qs", tag="qs", align_bytes=64)
+                pooled_rope(x, r, wide, wq_cs[h][0], wq_cs[h][1], qc[:], qs[:])
+                t_sb = soft.tile([P, NB], F32, name="t_sb", tag="t_sb")
+                for half in range(2):
+                    cols = slice(half * 512, (half + 1) * 512)
+                    sp = psum.tile([P, 512], F32, name="sp", tag="sp", bufs=2)
+                    nc.tensor.matmul_mx(out=sp[:], lhsT=qc[:].bitcast(FP8X4), lhsT_scale=qs[:], rhs=kc[:, cols].bitcast(FP8X4), rhs_scale=ks[:, cols], start=True, stop=True)
+                    nc.vector.tensor_tensor(out=t_sb[:, cols], in0=sp[:], in1=bias[:, cols], op=ALU.add)
+                mx = soft.tile([P, 1], F32, name="mx", tag="mx")
+                nc.vector.tensor_reduce(out=mx[:], in_=t_sb[:], axis=AX.X, op=ALU.max)
+                negm = soft.tile([P, 1], F32, name="negm", tag="negm")
+                nc.vector.tensor_scalar(out=negm[:], in0=mx[:], scalar1=-SCALE, scalar2=None, op0=ALU.mult)
+                e_sb = soft.tile([P, NB], F32, name="e_sb", tag="e_sb")
+                ssum = soft.tile([P, 1], F32, name="ssum", tag="ssum")
+                nc.scalar.activation(out=e_sb[:], in_=t_sb[:], func=ACT.Exp, bias=negm[:], scale=SCALE, accum_out=ssum[:])
+                rsum = soft.tile([P, 1], F32, name="rsum", tag="rsum")
+                nc.vector.reciprocal(out=rsum[:], in_=ssum[:])
+                o_sb = soft.tile([P, NB], F32, name="o_sb", tag="o_sb")
+                nc.scalar.activation(out=o_sb[:], in_=e_sb[:], func=ACT.Copy, scale=rsum[:])
+                nc.scalar.dma_start(out=out[0, h, r * P:(r + 1) * P, :], in_=o_sb[:])

@@ -15,7 +15,6 @@ ACT = mybir.ActivationFunctionType
 AX = mybir.AxisListType
 
 P = 128
-S_LEN = 16384
 D = 256
 HID = 512
 NB = 1024
@@ -26,30 +25,78 @@ BIG = 2.0 ** 35
 
 FLOPS = 2 * 3 * NB * HID * HID + 2 * 2 * NB * NB * HID
 
-WIDE16 = ((1, 1), (1, 3), (1, 5), (1, 7))
+PIN = False
+ROPE_ADD_ON_PE = True
+NORM = "gpsimd"
+WIDE_K = (0, 1, 2, 3)
+PF = 3
 
 
 def tile_attngate_t_kernel(tc, q, k, attention_mask, cos, sin, wq, wk, out):
     nc = tc.nc
     with ExitStack() as ctx:
         const = ctx.enter_context(tc.tile_pool(name="const", bufs=1))
-        xin = ctx.enter_context(tc.tile_pool(name="xin", bufs=4))
+        xin = ctx.enter_context(tc.tile_pool(name="xin", bufs=PF + 3))
         work = ctx.enter_context(tc.tile_pool(name="work", bufs=2))
         soft = ctx.enter_context(tc.tile_pool(name="soft", bufs=2))
         psum = ctx.enter_context(tc.psum_pool(name="psum", bufs=1))
+        if PIN:
+            ctx.enter_context(tc.manual_schedule())
+
+        chunks = [{"kind": "k", "h": 0, "r": r, "wide": r in WIDE_K, "src": k[0, 0]} for r in range(NR)]
+        chunks.extend([{"kind": "q", "h": h, "r": r, "wide": False, "src": q[0, h]} for r in range(NR) for h in range(2)])
+        n_chunks = len(chunks)
+        mask32 = attention_mask[0, 0].bitcast(I32).rearrange("(r p) w -> r p w", p=P)
+        mask_tiles = {}
+
+        def bank(i, shape, dtype, name):
+            return psum.tile(shape, dtype, name=name, tag="bank%d" % i)
+
+        def load_chunk(i):
+            st = chunks[i]
+            r = st["r"]
+            rows = st["src"][r * CHUNK:(r + 1) * CHUNK, :]
+            x = xin.tile([P, 4096], BF16, name="x", tag="x")
+            if st["wide"]:
+                nc.sync.dma_start(out=x[:].rearrange("p (g d) -> p g d", g=16), in_=rows.rearrange("(g p) d -> p g d", g=16, p=P))
+            else:
+                nc.sync.dma_start(out=x[:].rearrange("p (g e) -> p g e", g=8), in_=rows.rearrange("(g p l) d -> p g (l d)", g=8, p=P, l=2))
+            st["x"] = x
+            if st["kind"] == "q" and st["h"] == 0:
+                mraw = soft.tile([P, 2 * NB], I32, name="mraw", tag="mraw", bufs=3)
+                nc.sync.dma_start(out=mraw[:], in_=mask32[r])
+                mask_tiles[r] = {"raw": mraw}
+
+        def load_weight(w, name):
+            raw = const.tile([P, 4, HID], BF16, name="raw_" + name, tag="wraw", bufs=2)
+            nc.sync.dma_start(out=raw[:], in_=w.rearrange("(t p) n -> p t n", t=4, p=P))
+            return raw
+
+        def prep_weight(raw, name):
+            grouped = const.tile([P, HID, 4], BF16, name="grp_" + name, tag="wgrp", align_bytes=64)
+            nc.vector.tensor_copy(out=grouped[:], in_=raw[:].rearrange("p t n -> p n t"))
+            codes = const.tile([P, HID], U32, name="wc_" + name, align_bytes=64)
+            scales = const.tile([P, HID], U8, name="ws_" + name, align_bytes=64)
+            nc.vector.quantize_mx(out=codes[:].bitcast(FP8X4), scales=scales[:], in_=grouped[:].rearrange("p n t -> p (n t)"))
+            return codes, scales
+
+        load_chunk(0)
+        raw_k = load_weight(wk[0], "k")
+        load_chunk(1)
+        cos_sb = const.tile([P, NR, HID], BF16, name="cos_sb")
+        nc.sync.dma_start(out=cos_sb[:], in_=cos[0].rearrange("(r p) h -> p r h", p=P))
+        sin_sb = const.tile([P, NR, HID], BF16, name="sin_sb")
+        nc.sync.dma_start(out=sin_sb[:], in_=sin[0].rearrange("(r p) h -> p r h", p=P))
+        load_chunk(2)
 
         ident = const.tile([P, P], BF16, name="ident")
         make_identity(nc, ident[:])
+        identf = const.tile([P, P], F32, name="identf")
+        make_identity(nc, identf[:])
         perm8 = const.tile([P, P], BF16, name="perm8")
-        nc.vector.tensor_copy(
-            out=perm8[:].rearrange("p (h b) -> p h b", h=8),
-            in_=ident[:].rearrange("p (b h) -> p h b", h=8),
-        )
+        nc.vector.tensor_copy(out=perm8[:].rearrange("p (h b) -> p h b", h=8), in_=ident[:].rearrange("p (b h) -> p h b", h=8))
         perm16 = const.tile([P, P], BF16, name="perm16")
-        nc.vector.tensor_copy(
-            out=perm16[:].rearrange("p (h b) -> p h b", h=16),
-            in_=ident[:].rearrange("p (b h) -> p h b", h=16),
-        )
+        nc.vector.tensor_copy(out=perm16[:].rearrange("p (h b) -> p h b", h=16), in_=ident[:].rearrange("p (b h) -> p h b", h=16))
         cnt8 = const.tile([P, 16], F32, name="cnt8")
         nc.vector.tensor_reduce(out=cnt8[:], in_=ident[:].rearrange("p (n h) -> p n h", h=8), axis=AX.X, op=ALU.add)
         pool8 = const.tile([P, 16], BF16, name="pool8")
@@ -59,61 +106,60 @@ def tile_attngate_t_kernel(tc, q, k, attention_mask, cos, sin, wq, wk, out):
         pool16 = const.tile([P, 8], BF16, name="pool16")
         nc.vector.tensor_scalar(out=pool16[:], in0=cnt16[:], scalar1=1.0 / 16.0, scalar2=None, op0=ALU.mult)
 
-        def load_chunk(src, r, wide):
-            rows = src[r * CHUNK:(r + 1) * CHUNK, :]
-            x = xin.tile([P, 4096], BF16, name="x", tag="x")
-            if wide:
-                nc.sync.dma_start(out=x[:].rearrange("p (g d) -> p g d", g=16), in_=rows.rearrange("(g p) d -> p g d", g=16, p=P))
-            else:
-                nc.sync.dma_start(out=x[:].rearrange("p (g e) -> p g e", g=8), in_=rows.rearrange("(g p l) d -> p g (l d)", g=8, p=P, l=2))
-            return x
-
-        def load_weight(w, name):
-            raw = const.tile([P, 4, HID], BF16, name="raw_" + name)
-            nc.sync.dma_start(out=raw[:], in_=w.rearrange("(t p) n -> p t n", t=4, p=P))
-            grouped = const.tile([P, HID, 4], BF16, name="grp_" + name, align_bytes=64)
-            nc.vector.tensor_copy(out=grouped[:], in_=raw[:].rearrange("p t n -> p n t"))
-            codes = const.tile([P, HID], U32, name="wc_" + name, align_bytes=64)
-            scales = const.tile([P, HID], U8, name="ws_" + name, align_bytes=64)
-            nc.vector.quantize_mx(out=codes[:].bitcast(FP8X4), scales=scales[:], in_=grouped[:].rearrange("p n t -> p (n t)"))
-            return codes, scales
-
         kc = const.tile([P, NB], U32, name="kc", align_bytes=64)
         ks = const.tile([P, NB], U8, name="ks", align_bytes=64)
+        weights = {}
+        nsin_sb = const.tile([P, NR, 256], BF16, name="nsin_sb")
 
-        def pooled_rope(x, r, wide, wcodes, wscales, codes_out, scales_out):
-            groups = 16 if wide else 8
-            meanps = psum.tile([P, 2, P], F32, name="meanps", tag="mean")
-            first = work.tile([P, 2, groups, 64], BF16, name="first", tag="first%d" % groups)
-            if wide:
+        def st_sums(i):
+            st = chunks[i]
+            meanps = bank(0 if i % 2 == 0 else 7, [P, 2, P], F32, "meanps")
+            st["mean"] = meanps
+            x = st["x"]
+            if st["wide"]:
                 xv = x[:].rearrange("p (g d) -> p g d", g=16)
                 for g in range(16):
                     for c in range(2):
                         nc.tensor.matmul(out=meanps[:, c, g * 8:(g + 1) * 8], lhsT=xv[:, g, c * P:(c + 1) * P], rhs=pool16[:], start=True, stop=True)
-                src = xv
-                perm = perm16
             else:
                 xv = x[:].rearrange("p (g e) -> p g e", g=8)
                 for g in range(8):
                     for c in range(2):
                         for l in range(2):
-                            nc.tensor.matmul(
-                                out=meanps[:, c, g * 16:(g + 1) * 16],
-                                lhsT=xv[:, g, l * D + c * P:l * D + (c + 1) * P],
-                                rhs=pool8[:], start=(l == 0), stop=(l == 1),
-                            )
-                l1 = work.tile([P, 8, D], BF16, name="l1", tag="l1")
-                nc.vector.tensor_tensor(out=l1[:], in0=xv[:, :, 0:D], in1=xv[:, :, D:2 * D], op=ALU.max)
-                src = l1
-                perm = perm8
+                            nc.tensor.matmul(out=meanps[:, c, g * 16:(g + 1) * 16], lhsT=xv[:, g, l * D + c * P:l * D + (c + 1) * P], rhs=pool8[:], start=(l == 0), stop=(l == 1))
+
+        def st_l1(i):
+            st = chunks[i]
+            if st["wide"]:
+                st["tsrc"] = st["x"][:].rearrange("p (g d) -> p g d", g=16)
+                return
+            xv = st["x"][:].rearrange("p (g e) -> p g e", g=8)
+            l1 = work.tile([P, 8, D], BF16, name="l1", tag="l1")
+            nc.vector.tensor_tensor(out=l1[:], in0=xv[:, :, 0:D], in1=xv[:, :, D:2 * D], op=ALU.max)
+            st["tsrc"] = l1
+
+        def st_transpose(i):
+            st = chunks[i]
+            halves = 2 if st["wide"] else 1
+            perm = perm16 if st["wide"] else perm8
+            src = st["tsrc"]
+            st["tp"] = []
             for c in range(2):
-                for half in range(groups // 8):
-                    tp = psum.tile([P, 8, P], BF16, name="tp", tag="tp", bufs=3)
+                for half in range(halves):
+                    j = c * halves + half
+                    tp = bank(3 + j, [P, 8, P], BF16, "tp")
                     for g in range(8):
                         nc.tensor.transpose(out=tp[:, g, :], in_=src[:, half * 8 + g, c * P:(c + 1) * P], identity=perm[:])
-                    hi = work.tile([P, 8, 64], BF16, name="hi", tag="hi", bufs=3)
+                    hi = work.tile([P, 8, 64], BF16, name="hi", tag="hi%d" % j)
                     nc.scalar.copy(out=hi[:], in_=tp[:, :, 64:128])
-                    nc.vector.tensor_tensor(out=first[:, c, half * 8:(half + 1) * 8, :], in0=tp[:, :, 0:64], in1=hi[:], op=ALU.max)
+                    st["tp"].append((c, half, tp, hi))
+
+        def st_tree(i):
+            st = chunks[i]
+            groups = 16 if st["wide"] else 8
+            first = work.tile([P, 2, groups, 64], BF16, name="first", tag="first%d" % groups)
+            for c, half, tp, hi in st["tp"]:
+                nc.vector.tensor_tensor(out=first[:, c, half * 8:(half + 1) * 8, :], in0=tp[:, :, 0:64], in1=hi[:], op=ALU.max)
             cur = first
             width = 64
             while width > P // groups:
@@ -122,67 +168,142 @@ def tile_attngate_t_kernel(tc, q, k, attention_mask, cos, sin, wq, wk, out):
                 nc.vector.tensor_tensor(out=nxt[:], in0=cur[:, :, :, 0:width], in1=cur[:, :, :, width:2 * width], op=ALU.max)
                 cur = nxt
             grp = work.tile([P, P, 4], BF16, name="grp", tag="grp", align_bytes=64)
-            nc.scalar.copy(out=grp[:, :, 0:2], in_=meanps[:].rearrange("p c b -> p b c"))
+            nc.scalar.copy(out=grp[:, :, 0:2], in_=st["mean"][:].rearrange("p c b -> p b c"))
             nc.scalar.copy(out=grp[:, :, 2:4], in_=cur[:].rearrange("p c g b -> p (g b) c"))
+            st["grp"] = grp
+
+        def st_project(i):
+            st = chunks[i]
             pc = work.tile([P, P], U32, name="pc", tag="pc", align_bytes=64)
             pscale = work.tile([P, P], U8, name="pscale", tag="pscale", align_bytes=64)
-            nc.vector.quantize_mx(out=pc[:].bitcast(FP8X4), scales=pscale[:], in_=grp[:].rearrange("p b t -> p (b t)"))
-            xps = psum.tile([P, HID], F32, name="xps", tag="xps")
+            nc.vector.quantize_mx(out=pc[:].bitcast(FP8X4), scales=pscale[:], in_=st["grp"][:].rearrange("p b t -> p (b t)"))
+            wcodes, wscales = weights[(st["kind"], st["h"])]
+            xps = bank(1, [P, HID], F32, "xps")
             nc.tensor.matmul_mx(out=xps[:], lhsT=pc[:].bitcast(FP8X4), lhsT_scale=pscale[:], rhs=wcodes[:].bitcast(FP8X4), rhs_scale=wscales[:], start=True, stop=True)
+            st["xps"] = xps
+
+        def st_rope(i):
+            st = chunks[i]
+            r = st["r"]
+            xps = st["xps"]
             m1 = work.tile([P, HID], F32, name="m1", tag="m1")
             nc.vector.tensor_tensor(out=m1[:], in0=xps[:], in1=cos_sb[:, r, :], op=ALU.mult)
             m2 = work.tile([P, HID], F32, name="m2", tag="m2")
             nc.vector.tensor_tensor(out=m2[:, 0:256], in0=xps[:, 256:512], in1=nsin_sb[:, r, :], op=ALU.mult)
             nc.vector.tensor_tensor(out=m2[:, 256:512], in0=xps[:, 0:256], in1=sin_sb[:, r, 256:512], op=ALU.mult)
-            y = work.tile([P, HID], BF16, name="y", tag="y")
-            nc.vector.tensor_tensor(out=y[:], in0=m1[:], in1=m2[:], op=ALU.add)
-            yt = psum.tile([P, 4, P], BF16, name="yt", tag="yt")
-            for t in range(4):
-                nc.tensor.transpose(out=yt[:, t, :], in_=y[:, t * P:(t + 1) * P], identity=ident[:])
+            if ROPE_ADD_ON_PE:
+                yt = bank(2, [P, 4, P], F32, "yt")
+                for t in range(4):
+                    nc.tensor.matmul(out=yt[:, t, :], lhsT=m1[:, t * P:(t + 1) * P], rhs=identf[:], is_transpose=True, start=True, stop=False)
+                    nc.tensor.matmul(out=yt[:, t, :], lhsT=m2[:, t * P:(t + 1) * P], rhs=identf[:], is_transpose=True, start=False, stop=True)
+            else:
+                y = work.tile([P, HID], BF16, name="y", tag="y")
+                nc.vector.tensor_tensor(out=y[:], in0=m1[:], in1=m2[:], op=ALU.add)
+                yt = bank(2, [P, 4, P], BF16, "yt")
+                for t in range(4):
+                    nc.tensor.transpose(out=yt[:, t, :], in_=y[:, t * P:(t + 1) * P], identity=ident[:])
             g2 = work.tile([P, P, 4], BF16, name="g2", tag="g2", align_bytes=64)
             nc.scalar.copy(out=g2[:], in_=yt[:].rearrange("p t b -> p b t"))
-            nc.vector.quantize_mx(out=codes_out.bitcast(FP8X4), scales=scales_out, in_=g2[:].rearrange("p b t -> p (b t)"))
+            st["g2"] = g2
 
-        x0 = load_chunk(k[0, 0], 0, False)
-        wk_c, wk_s = load_weight(wk[0], "k")
-        cos_sb = const.tile([P, NR, HID], BF16, name="cos_sb")
-        nc.sync.dma_start(out=cos_sb[:], in_=cos[0].rearrange("(r p) h -> p r h", p=P))
-        sin_sb = const.tile([P, NR, HID], BF16, name="sin_sb")
-        nc.sync.dma_start(out=sin_sb[:], in_=sin[0].rearrange("(r p) h -> p r h", p=P))
-        nsin_sb = const.tile([P, NR, 256], BF16, name="nsin_sb")
-        nc.vector.tensor_scalar(out=nsin_sb[:], in0=sin_sb[:, :, 0:256], scalar1=-1.0, scalar2=None, op0=ALU.mult)
-        for r in range(NR):
-            x = x0 if r == 0 else load_chunk(k[0, 0], r, False)
-            pooled_rope(x, r, False, wk_c, wk_s, kc[:, r * P:(r + 1) * P], ks[:, r * P:(r + 1) * P])
-        wq_cs = [load_weight(wq[h], "q%d" % h) for h in range(2)]
+        def st_scores(i):
+            st = chunks[i]
+            r = st["r"]
+            g2v = st["g2"][:].rearrange("p b t -> p (b t)")
+            if st["kind"] == "k":
+                nc.vector.quantize_mx(out=kc[:, r * P:(r + 1) * P].bitcast(FP8X4), scales=ks[:, r * P:(r + 1) * P], in_=g2v)
+                return
+            qc = work.tile([P, P], U32, name="qc", tag="qc", align_bytes=64)
+            qs = work.tile([P, P], U8, name="qs", tag="qs", align_bytes=64)
+            nc.vector.quantize_mx(out=qc[:].bitcast(FP8X4), scales=qs[:], in_=g2v)
+            st["sp"] = []
+            for half in range(2):
+                cols = slice(half * 512, (half + 1) * 512)
+                sp = bank(5 + half, [P, 512], F32, "sp")
+                nc.tensor.matmul_mx(out=sp[:], lhsT=qc[:].bitcast(FP8X4), lhsT_scale=qs[:], rhs=kc[:, cols].bitcast(FP8X4), rhs_scale=ks[:, cols], start=True, stop=True)
+                st["sp"].append(sp)
 
-        mask32 = attention_mask[0, 0].bitcast(I32).rearrange("(r p) w -> r p w", p=P)
-        for r in range(NR):
-            mraw = soft.tile([P, 2 * NB], I32, name="mraw", tag="mraw")
-            nc.sync.dma_start(out=mraw[:], in_=mask32[r])
-            bias = soft.tile([P, NB], BF16, name="bias", tag="bias")
-            nc.scalar.activation(out=bias[:], in_=mraw[:].bitcast(U32).rearrange("p (w two) -> p w two", two=2)[:, :, 0], func=ACT.Copy, bias=-BIG, scale=BIG)
-            for h in range(2):
-                wide = (h, r) in WIDE16
-                x = load_chunk(q[0, h], r, wide)
-                qc = work.tile([P, P], U32, name="qc", tag="qc", align_bytes=64)
-                qs = work.tile([P, P], U8, name="qs", tag="qs", align_bytes=64)
-                pooled_rope(x, r, wide, wq_cs[h][0], wq_cs[h][1], qc[:], qs[:])
-                t_sb = soft.tile([P, NB], F32, name="t_sb", tag="t_sb")
-                for half in range(2):
-                    cols = slice(half * 512, (half + 1) * 512)
-                    sp = psum.tile([P, 512], F32, name="sp", tag="sp", bufs=2)
-                    nc.tensor.matmul_mx(out=sp[:], lhsT=qc[:].bitcast(FP8X4), lhsT_scale=qs[:], rhs=kc[:, cols].bitcast(FP8X4), rhs_scale=ks[:, cols], start=True, stop=True)
-                    nc.vector.tensor_tensor(out=t_sb[:, cols], in0=sp[:], in1=bias[:, cols], op=ALU.add)
-                mx = soft.tile([P, 1], F32, name="mx", tag="mx")
-                nc.vector.tensor_reduce(out=mx[:], in_=t_sb[:], axis=AX.X, op=ALU.max)
-                negm = soft.tile([P, 1], F32, name="negm", tag="negm")
-                nc.vector.tensor_scalar(out=negm[:], in0=mx[:], scalar1=-SCALE, scalar2=None, op0=ALU.mult)
-                e_sb = soft.tile([P, NB], F32, name="e_sb", tag="e_sb")
-                ssum = soft.tile([P, 1], F32, name="ssum", tag="ssum")
-                nc.scalar.activation(out=e_sb[:], in_=t_sb[:], func=ACT.Exp, bias=negm[:], scale=SCALE, accum_out=ssum[:])
-                rsum = soft.tile([P, 1], F32, name="rsum", tag="rsum")
-                nc.vector.reciprocal(out=rsum[:], in_=ssum[:])
-                o_sb = soft.tile([P, NB], F32, name="o_sb", tag="o_sb")
-                nc.scalar.activation(out=o_sb[:], in_=e_sb[:], func=ACT.Copy, scale=rsum[:])
-                nc.scalar.dma_start(out=out[0, h, r * P:(r + 1) * P, :], in_=o_sb[:])
+        def st_mask(r):
+            bias = soft.tile([P, NB], BF16, name="bias", tag="bias", bufs=3)
+            nc.scalar.activation(out=bias[:], in_=mask_tiles[r]["raw"][:].bitcast(U32).rearrange("p (w two) -> p w two", two=2)[:, :, 0], func=ACT.Copy, bias=-BIG, scale=BIG)
+            mask_tiles[r]["bias"] = bias
+
+        def st_softmax(i):
+            st = chunks[i]
+            bias = mask_tiles[st["r"]]["bias"]
+            t_sb = soft.tile([P, NB], F32, name="t_sb", tag="t_sb")
+            for half in range(2):
+                cols = slice(half * 512, (half + 1) * 512)
+                nc.vector.tensor_tensor(out=t_sb[:, cols], in0=st["sp"][half][:], in1=bias[:, cols], op=ALU.add)
+            mx = soft.tile([P, 1], F32, name="mx", tag="mx")
+            nc.vector.tensor_reduce(out=mx[:], in_=t_sb[:], axis=AX.X, op=ALU.max)
+            negm = soft.tile([P, 1], F32, name="negm", tag="negm")
+            nc.vector.tensor_scalar(out=negm[:], in0=mx[:], scalar1=-SCALE, scalar2=None, op0=ALU.mult)
+            e_sb = soft.tile([P, NB], F32, name="e_sb", tag="e_sb")
+            ssum = soft.tile([P, 1], F32, name="ssum", tag="ssum")
+            nc.scalar.activation(out=e_sb[:], in_=t_sb[:], func=ACT.Exp, bias=negm[:], scale=SCALE, accum_out=ssum[:])
+            st["e"] = e_sb
+            st["ssum"] = ssum
+
+        def st_norm(i):
+            st = chunks[i]
+            rsum = soft.tile([P, 1], F32, name="rsum", tag="rsum")
+            nc.vector.reciprocal(out=rsum[:], in_=st["ssum"][:])
+            o_sb = soft.tile([P, NB], F32, name="o_sb", tag="o_sb", bufs=3)
+            if NORM == "gpsimd":
+                nc.gpsimd.tensor_scalar(out=o_sb[:], in0=st["e"][:], scalar1=rsum[:], scalar2=0.0, op0=ALU.mult, op1=ALU.add)
+            elif NORM == "scalar":
+                nc.scalar.activation(out=o_sb[:], in_=st["e"][:], func=ACT.Copy, scale=rsum[:])
+            else:
+                nc.vector.tensor_scalar(out=o_sb[:], in0=st["e"][:], scalar1=rsum[:], scalar2=None, op0=ALU.mult)
+            st["o"] = o_sb
+
+        def st_store(i):
+            st = chunks[i]
+            r = st["r"]
+            nc.sync.dma_start(out=out[0, st["h"], r * P:(r + 1) * P, :], in_=st["o"][:])
+
+        def is_q(i):
+            return 0 <= i < n_chunks and chunks[i]["kind"] == "q"
+
+        def valid(i):
+            return 0 <= i < n_chunks
+
+        raws = {}
+        for n in range(n_chunks + 8):
+            if is_q(n - 6):
+                st_norm(n - 6)
+            if is_q(n - 7):
+                st_store(n - 7)
+            if valid(n - 1):
+                st_transpose(n - 1)
+            if valid(n + PF):
+                load_chunk(n + PF)
+            if n == 2:
+                raws[0] = load_weight(wq[0], "q0")
+            if n == 3:
+                raws[1] = load_weight(wq[1], "q1")
+            if valid(n):
+                st_sums(n)
+            if n == 0:
+                weights[("k", 0)] = prep_weight(raw_k, "k")
+            if n == 5:
+                weights[("q", 0)] = prep_weight(raws[0], "q0")
+            if n == 6:
+                weights[("q", 1)] = prep_weight(raws[1], "q1")
+            if is_q(n - 2) and chunks[n - 2]["h"] == 0:
+                st_mask(chunks[n - 2]["r"])
+            if is_q(n - 5):
+                st_softmax(n - 5)
+            if valid(n - 3):
+                st_rope(n - 3)
+            if valid(n - 1):
+                st_tree(n - 1)
+            if n == 2:
+                nc.vector.tensor_scalar(out=nsin_sb[:], in0=sin_sb[:, :, 0:256], scalar1=-1.0, scalar2=None, op0=ALU.mult)
+            if valid(n - 2):
+                st_project(n - 2)
+            if valid(n - 4):
+                st_scores(n - 4)
+            if valid(n):
+                st_l1(n)

@@ -25,11 +25,14 @@ BIG = 2.0 ** 35
 
 FLOPS = 2 * 3 * NB * HID * HID + 2 * 2 * NB * NB * HID
 
-PIN = False
+PIN = True
 ROPE_ADD_ON_PE = True
 NORM = "gpsimd"
-WIDE_K = (0, 1, 2, 3)
+WIDE_K = (2, 3, 4, 5)
 PF = 3
+LEAD = 2
+STORE = "gpsimd"
+TAIL_V = 2
 
 
 def tile_attngate_t_kernel(tc, q, k, attention_mask, cos, sin, wq, wk, out):
@@ -62,13 +65,17 @@ def tile_attngate_t_kernel(tc, q, k, attention_mask, cos, sin, wq, wk, out):
             else:
                 nc.sync.dma_start(out=x[:].rearrange("p (g e) -> p g e", g=8), in_=rows.rearrange("(g p l) d -> p g (l d)", g=8, p=P, l=2))
             st["x"] = x
-            if st["kind"] == "q" and st["h"] == 0:
-                mraw = soft.tile([P, 2 * NB], I32, name="mraw", tag="mraw", bufs=3)
-                nc.sync.dma_start(out=mraw[:], in_=mask32[r])
-                mask_tiles[r] = {"raw": mraw}
+            if st["kind"] == "k":
+                nc.sync.dma_start(out=cos_sb[:, r, :], in_=cos[0, r * P:(r + 1) * P, :])
+                nc.sync.dma_start(out=sin_sb[:, r, :], in_=sin[0, r * P:(r + 1) * P, :])
+
+        def load_mask(r):
+            mraw = soft.tile([P, 2 * NB], I32, name="mraw", tag="mraw", bufs=3)
+            nc.sync.dma_start(out=mraw[:], in_=mask32[r])
+            mask_tiles[r] = {"raw": mraw}
 
         def load_weight(w, name):
-            raw = const.tile([P, 4, HID], BF16, name="raw_" + name, tag="wraw", bufs=2)
+            raw = const.tile([P, 4, HID], BF16, name="raw_" + name, tag="wraw", bufs=3)
             nc.sync.dma_start(out=raw[:], in_=w.rearrange("(t p) n -> p t n", t=4, p=P))
             return raw
 
@@ -80,14 +87,13 @@ def tile_attngate_t_kernel(tc, q, k, attention_mask, cos, sin, wq, wk, out):
             nc.vector.quantize_mx(out=codes[:].bitcast(FP8X4), scales=scales[:], in_=grouped[:].rearrange("p n t -> p (n t)"))
             return codes, scales
 
+        cos_sb = const.tile([P, NR, HID], BF16, name="cos_sb")
+        sin_sb = const.tile([P, NR, HID], BF16, name="sin_sb")
+        nsin_sb = const.tile([P, NR, 256], BF16, name="nsin_sb")
         load_chunk(0)
         raw_k = load_weight(wk[0], "k")
-        load_chunk(1)
-        cos_sb = const.tile([P, NR, HID], BF16, name="cos_sb")
-        nc.sync.dma_start(out=cos_sb[:], in_=cos[0].rearrange("(r p) h -> p r h", p=P))
-        sin_sb = const.tile([P, NR, HID], BF16, name="sin_sb")
-        nc.sync.dma_start(out=sin_sb[:], in_=sin[0].rearrange("(r p) h -> p r h", p=P))
-        load_chunk(2)
+        for i in range(1, PF):
+            load_chunk(i)
 
         ident = const.tile([P, P], BF16, name="ident")
         make_identity(nc, ident[:])
@@ -109,7 +115,8 @@ def tile_attngate_t_kernel(tc, q, k, attention_mask, cos, sin, wq, wk, out):
         kc = const.tile([P, NB], U32, name="kc", align_bytes=64)
         ks = const.tile([P, NB], U8, name="ks", align_bytes=64)
         weights = {}
-        nsin_sb = const.tile([P, NR, 256], BF16, name="nsin_sb")
+        qc_all = const.tile([P, 2 * NR, P], U32, name="qc_all", align_bytes=64)
+        qs_all = const.tile([P, 2 * NR, P], U8, name="qs_all", align_bytes=64)
 
         def st_sums(i):
             st = chunks[i]
@@ -154,22 +161,32 @@ def tile_attngate_t_kernel(tc, q, k, attention_mask, cos, sin, wq, wk, out):
                     nc.scalar.copy(out=hi[:], in_=tp[:, :, 64:128])
                     st["tp"].append((c, half, tp, hi))
 
-        def st_tree(i):
+        def st_tree_first(i):
             st = chunks[i]
             groups = 16 if st["wide"] else 8
             first = work.tile([P, 2, groups, 64], BF16, name="first", tag="first%d" % groups)
             for c, half, tp, hi in st["tp"]:
                 nc.vector.tensor_tensor(out=first[:, c, half * 8:(half + 1) * 8, :], in0=tp[:, :, 0:64], in1=hi[:], op=ALU.max)
-            cur = first
-            width = 64
-            while width > P // groups:
-                width = width // 2
-                nxt = work.tile([P, 2, groups, width], BF16, name="lvl", tag="lvl%d_%d" % (groups, width))
-                nc.vector.tensor_tensor(out=nxt[:], in0=cur[:, :, :, 0:width], in1=cur[:, :, :, width:2 * width], op=ALU.max)
-                cur = nxt
+            st["cur"] = first
+            st["width"] = 64
+
+        def st_tree_level(i):
+            st = chunks[i]
+            groups = 16 if st["wide"] else 8
+            if st["width"] == P // groups:
+                return
+            width = st["width"] // 2
+            cur = st["cur"]
+            nxt = work.tile([P, 2, groups, width], BF16, name="lvl", tag="lvl%d_%d" % (groups, width))
+            nc.vector.tensor_tensor(out=nxt[:], in0=cur[:, :, :, 0:width], in1=cur[:, :, :, width:2 * width], op=ALU.max)
+            st["cur"] = nxt
+            st["width"] = width
+
+        def st_regroup(i):
+            st = chunks[i]
             grp = work.tile([P, P, 4], BF16, name="grp", tag="grp", align_bytes=64)
             nc.scalar.copy(out=grp[:, :, 0:2], in_=st["mean"][:].rearrange("p c b -> p b c"))
-            nc.scalar.copy(out=grp[:, :, 2:4], in_=cur[:].rearrange("p c g b -> p (g b) c"))
+            nc.scalar.copy(out=grp[:, :, 2:4], in_=st["cur"][:].rearrange("p c g b -> p (g b) c"))
             st["grp"] = grp
 
         def st_project(i):
@@ -182,15 +199,25 @@ def tile_attngate_t_kernel(tc, q, k, attention_mask, cos, sin, wq, wk, out):
             nc.tensor.matmul_mx(out=xps[:], lhsT=pc[:].bitcast(FP8X4), lhsT_scale=pscale[:], rhs=wcodes[:].bitcast(FP8X4), rhs_scale=wscales[:], start=True, stop=True)
             st["xps"] = xps
 
-        def st_rope(i):
+        def st_rope_a(i):
             st = chunks[i]
-            r = st["r"]
-            xps = st["xps"]
+            if st["kind"] == "k":
+                nc.vector.tensor_scalar(out=nsin_sb[:, st["r"], :], in0=sin_sb[:, st["r"], 0:256], scalar1=-1.0, scalar2=None, op0=ALU.mult)
             m1 = work.tile([P, HID], F32, name="m1", tag="m1")
-            nc.vector.tensor_tensor(out=m1[:], in0=xps[:], in1=cos_sb[:, r, :], op=ALU.mult)
+            nc.vector.tensor_tensor(out=m1[:], in0=st["xps"][:], in1=cos_sb[:, st["r"], :], op=ALU.mult)
+            st["m1"] = m1
+
+        def st_rope_b(i):
+            st = chunks[i]
             m2 = work.tile([P, HID], F32, name="m2", tag="m2")
-            nc.vector.tensor_tensor(out=m2[:, 0:256], in0=xps[:, 256:512], in1=nsin_sb[:, r, :], op=ALU.mult)
-            nc.vector.tensor_tensor(out=m2[:, 256:512], in0=xps[:, 0:256], in1=sin_sb[:, r, 256:512], op=ALU.mult)
+            nc.vector.tensor_tensor(out=m2[:, 0:256], in0=st["xps"][:, 256:512], in1=nsin_sb[:, st["r"], :], op=ALU.mult)
+            st["m2"] = m2
+
+        def st_rope_c(i):
+            st = chunks[i]
+            m1 = st["m1"]
+            m2 = st["m2"]
+            nc.vector.tensor_tensor(out=m2[:, 256:512], in0=st["xps"][:, 0:256], in1=sin_sb[:, st["r"], 256:512], op=ALU.mult)
             if ROPE_ADD_ON_PE:
                 yt = bank(2, [P, 4, P], F32, "yt")
                 for t in range(4):
@@ -206,21 +233,22 @@ def tile_attngate_t_kernel(tc, q, k, attention_mask, cos, sin, wq, wk, out):
             nc.scalar.copy(out=g2[:], in_=yt[:].rearrange("p t b -> p b t"))
             st["g2"] = g2
 
-        def st_scores(i):
+        def st_quant2(i):
             st = chunks[i]
             r = st["r"]
             g2v = st["g2"][:].rearrange("p b t -> p (b t)")
             if st["kind"] == "k":
                 nc.vector.quantize_mx(out=kc[:, r * P:(r + 1) * P].bitcast(FP8X4), scales=ks[:, r * P:(r + 1) * P], in_=g2v)
-                return
-            qc = work.tile([P, P], U32, name="qc", tag="qc", align_bytes=64)
-            qs = work.tile([P, P], U8, name="qs", tag="qs", align_bytes=64)
-            nc.vector.quantize_mx(out=qc[:].bitcast(FP8X4), scales=qs[:], in_=g2v)
+            else:
+                nc.vector.quantize_mx(out=qc_all[:, i - NR, :].bitcast(FP8X4), scales=qs_all[:, i - NR, :], in_=g2v)
+
+        def st_scores(i):
+            st = chunks[i]
             st["sp"] = []
             for half in range(2):
                 cols = slice(half * 512, (half + 1) * 512)
                 sp = bank(5 + half, [P, 512], F32, "sp")
-                nc.tensor.matmul_mx(out=sp[:], lhsT=qc[:].bitcast(FP8X4), lhsT_scale=qs[:], rhs=kc[:, cols].bitcast(FP8X4), rhs_scale=ks[:, cols], start=True, stop=True)
+                nc.tensor.matmul_mx(out=sp[:], lhsT=qc_all[:, i - NR, :].bitcast(FP8X4), lhsT_scale=qs_all[:, i - NR, :], rhs=kc[:, cols].bitcast(FP8X4), rhs_scale=ks[:, cols], start=True, stop=True)
                 st["sp"].append(sp)
 
         def st_mask(r):
@@ -228,20 +256,28 @@ def tile_attngate_t_kernel(tc, q, k, attention_mask, cos, sin, wq, wk, out):
             nc.scalar.activation(out=bias[:], in_=mask_tiles[r]["raw"][:].bitcast(U32).rearrange("p (w two) -> p w two", two=2)[:, :, 0], func=ACT.Copy, bias=-BIG, scale=BIG)
             mask_tiles[r]["bias"] = bias
 
-        def st_softmax(i):
+        def st_soft_add(i):
             st = chunks[i]
             bias = mask_tiles[st["r"]]["bias"]
-            t_sb = soft.tile([P, NB], F32, name="t_sb", tag="t_sb")
+            t_sb = soft.tile([P, NB], F32, name="t_sb", tag="t_sb", bufs=3)
             for half in range(2):
                 cols = slice(half * 512, (half + 1) * 512)
                 nc.vector.tensor_tensor(out=t_sb[:, cols], in0=st["sp"][half][:], in1=bias[:, cols], op=ALU.add)
+            st["t"] = t_sb
+
+        def st_soft_max(i):
+            st = chunks[i]
             mx = soft.tile([P, 1], F32, name="mx", tag="mx")
-            nc.vector.tensor_reduce(out=mx[:], in_=t_sb[:], axis=AX.X, op=ALU.max)
+            nc.vector.tensor_reduce(out=mx[:], in_=st["t"][:], axis=AX.X, op=ALU.max)
+            st["mx"] = mx
+
+        def st_soft_exp(i):
+            st = chunks[i]
             negm = soft.tile([P, 1], F32, name="negm", tag="negm")
-            nc.vector.tensor_scalar(out=negm[:], in0=mx[:], scalar1=-SCALE, scalar2=None, op0=ALU.mult)
+            nc.vector.tensor_scalar(out=negm[:], in0=st["mx"][:], scalar1=-SCALE, scalar2=None, op0=ALU.mult)
             e_sb = soft.tile([P, NB], F32, name="e_sb", tag="e_sb")
             ssum = soft.tile([P, 1], F32, name="ssum", tag="ssum")
-            nc.scalar.activation(out=e_sb[:], in_=t_sb[:], func=ACT.Exp, bias=negm[:], scale=SCALE, accum_out=ssum[:])
+            nc.scalar.activation(out=e_sb[:], in_=st["t"][:], func=ACT.Exp, bias=negm[:], scale=SCALE, accum_out=ssum[:])
             st["e"] = e_sb
             st["ssum"] = ssum
 
@@ -250,7 +286,7 @@ def tile_attngate_t_kernel(tc, q, k, attention_mask, cos, sin, wq, wk, out):
             rsum = soft.tile([P, 1], F32, name="rsum", tag="rsum")
             nc.vector.reciprocal(out=rsum[:], in_=st["ssum"][:])
             o_sb = soft.tile([P, NB], F32, name="o_sb", tag="o_sb", bufs=3)
-            if NORM == "gpsimd":
+            if NORM == "gpsimd" and i < n_chunks - TAIL_V:
                 nc.gpsimd.tensor_scalar(out=o_sb[:], in0=st["e"][:], scalar1=rsum[:], scalar2=0.0, op0=ALU.mult, op1=ALU.add)
             elif NORM == "scalar":
                 nc.scalar.activation(out=o_sb[:], in_=st["e"][:], func=ACT.Copy, scale=rsum[:])
@@ -261,7 +297,10 @@ def tile_attngate_t_kernel(tc, q, k, attention_mask, cos, sin, wq, wk, out):
         def st_store(i):
             st = chunks[i]
             r = st["r"]
-            nc.sync.dma_start(out=out[0, st["h"], r * P:(r + 1) * P, :], in_=st["o"][:])
+            if STORE == "gpsimd":
+                nc.gpsimd.dma_start(out=out[0, st["h"], r * P:(r + 1) * P, :], in_=st["o"][:])
+            else:
+                nc.sync.dma_start(out=out[0, st["h"], r * P:(r + 1) * P, :], in_=st["o"][:])
 
         def is_q(i):
             return 0 <= i < n_chunks and chunks[i]["kind"] == "q"
@@ -270,40 +309,56 @@ def tile_attngate_t_kernel(tc, q, k, attention_mask, cos, sin, wq, wk, out):
             return 0 <= i < n_chunks
 
         raws = {}
-        for n in range(n_chunks + 8):
-            if is_q(n - 6):
-                st_norm(n - 6)
-            if is_q(n - 7):
-                st_store(n - 7)
-            if valid(n - 1):
-                st_transpose(n - 1)
+        for n in range(n_chunks + 9 + LEAD):
+            s = n - LEAD
             if valid(n + PF):
                 load_chunk(n + PF)
-            if n == 2:
+            if n == 0:
                 raws[0] = load_weight(wq[0], "q0")
-            if n == 3:
+            if n == 1:
                 raws[1] = load_weight(wq[1], "q1")
+            if is_q(s + 1) and chunks[s + 1]["h"] == 0:
+                load_mask(chunks[s + 1]["r"])
             if valid(n):
                 st_sums(n)
+                st_l1(n)
             if n == 0:
                 weights[("k", 0)] = prep_weight(raw_k, "k")
-            if n == 5:
-                weights[("q", 0)] = prep_weight(raws[0], "q0")
-            if n == 6:
-                weights[("q", 1)] = prep_weight(raws[1], "q1")
-            if is_q(n - 2) and chunks[n - 2]["h"] == 0:
-                st_mask(chunks[n - 2]["r"])
-            if is_q(n - 5):
-                st_softmax(n - 5)
-            if valid(n - 3):
-                st_rope(n - 3)
+            if is_q(s - 2) and chunks[s - 2]["h"] == 0:
+                st_mask(chunks[s - 2]["r"])
+            if is_q(s - 5):
+                st_soft_add(s - 5)
+            if is_q(s - 4):
+                st_scores(s - 4)
             if valid(n - 1):
-                st_tree(n - 1)
-            if n == 2:
-                nc.vector.tensor_scalar(out=nsin_sb[:], in0=sin_sb[:, :, 0:256], scalar1=-1.0, scalar2=None, op0=ALU.mult)
+                st_tree_first(n - 1)
+            if valid(n):
+                st_transpose(n)
+            if is_q(s - 6):
+                st_soft_max(s - 6)
+            if valid(n - 3):
+                st_rope_a(n - 3)
+            if is_q(s - 7):
+                st_norm(s - 7)
+                st_store(s - 7)
+            if valid(n - 1):
+                st_tree_level(n - 1)
+            if is_q(s - 6):
+                st_soft_exp(s - 6)
+            if valid(n - 3):
+                st_rope_b(n - 3)
+            if valid(n - 1):
+                st_tree_level(n - 1)
+            if valid(n - 3):
+                st_rope_c(n - 3)
+            if n == 3:
+                weights[("q", 0)] = prep_weight(raws[0], "q0")
+            if n == 4:
+                weights[("q", 1)] = prep_weight(raws[1], "q1")
+            if valid(n - 1):
+                st_tree_level(n - 1)
+                st_regroup(n - 1)
             if valid(n - 2):
                 st_project(n - 2)
             if valid(n - 4):
-                st_scores(n - 4)
-            if valid(n):
-                st_l1(n)
+                st_quant2(n - 4)

@@ -25,14 +25,13 @@ BIG = 2.0 ** 35
 
 FLOPS = 2 * 3 * NB * HID * HID + 2 * 2 * NB * NB * HID
 
-PIN = True
+PIN = False
 ROPE_ADD_ON_PE = True
 NORM = "gpsimd"
-WIDE_K = (2, 3, 4, 5)
+WIDE_K = (0, 1, 2, 3)
 PF = 3
-LEAD = 2
-STORE = "gpsimd"
-TAIL_V = 2
+FUEL_S = 2
+FUEL_P = 2
 
 
 def tile_attngate_t_kernel(tc, q, k, attention_mask, cos, sin, wq, wk, out):
@@ -65,17 +64,13 @@ def tile_attngate_t_kernel(tc, q, k, attention_mask, cos, sin, wq, wk, out):
             else:
                 nc.sync.dma_start(out=x[:].rearrange("p (g e) -> p g e", g=8), in_=rows.rearrange("(g p l) d -> p g (l d)", g=8, p=P, l=2))
             st["x"] = x
-            if st["kind"] == "k":
-                nc.sync.dma_start(out=cos_sb[:, r, :], in_=cos[0, r * P:(r + 1) * P, :])
-                nc.sync.dma_start(out=sin_sb[:, r, :], in_=sin[0, r * P:(r + 1) * P, :])
-
-        def load_mask(r):
-            mraw = soft.tile([P, 2 * NB], I32, name="mraw", tag="mraw", bufs=3)
-            nc.sync.dma_start(out=mraw[:], in_=mask32[r])
-            mask_tiles[r] = {"raw": mraw}
+            if st["kind"] == "q" and st["h"] == 0:
+                mraw = soft.tile([P, 2 * NB], I32, name="mraw", tag="mraw", bufs=3)
+                nc.sync.dma_start(out=mraw[:], in_=mask32[r])
+                mask_tiles[r] = {"raw": mraw}
 
         def load_weight(w, name):
-            raw = const.tile([P, 4, HID], BF16, name="raw_" + name, tag="wraw", bufs=3)
+            raw = const.tile([P, 4, HID], BF16, name="raw_" + name, tag="wraw", bufs=2)
             nc.sync.dma_start(out=raw[:], in_=w.rearrange("(t p) n -> p t n", t=4, p=P))
             return raw
 
@@ -87,13 +82,14 @@ def tile_attngate_t_kernel(tc, q, k, attention_mask, cos, sin, wq, wk, out):
             nc.vector.quantize_mx(out=codes[:].bitcast(FP8X4), scales=scales[:], in_=grouped[:].rearrange("p n t -> p (n t)"))
             return codes, scales
 
-        cos_sb = const.tile([P, NR, HID], BF16, name="cos_sb")
-        sin_sb = const.tile([P, NR, HID], BF16, name="sin_sb")
-        nsin_sb = const.tile([P, NR, 256], BF16, name="nsin_sb")
         load_chunk(0)
         raw_k = load_weight(wk[0], "k")
-        for i in range(1, PF):
-            load_chunk(i)
+        load_chunk(1)
+        cos_sb = const.tile([P, NR, HID], BF16, name="cos_sb")
+        nc.sync.dma_start(out=cos_sb[:], in_=cos[0].rearrange("(r p) h -> p r h", p=P))
+        sin_sb = const.tile([P, NR, HID], BF16, name="sin_sb")
+        nc.sync.dma_start(out=sin_sb[:], in_=sin[0].rearrange("(r p) h -> p r h", p=P))
+        load_chunk(2)
 
         ident = const.tile([P, P], BF16, name="ident")
         make_identity(nc, ident[:])
@@ -115,8 +111,12 @@ def tile_attngate_t_kernel(tc, q, k, attention_mask, cos, sin, wq, wk, out):
         kc = const.tile([P, NB], U32, name="kc", align_bytes=64)
         ks = const.tile([P, NB], U8, name="ks", align_bytes=64)
         weights = {}
-        qc_all = const.tile([P, 2 * NR, P], U32, name="qc_all", align_bytes=64)
-        qs_all = const.tile([P, 2 * NR, P], U8, name="qs_all", align_bytes=64)
+        nsin_sb = const.tile([P, NR, 256], BF16, name="nsin_sb")
+
+        def fuel(target, count):
+            wcodes, wscales = weights[("k", 0)]
+            for j in range(count):
+                nc.tensor.matmul_mx(out=target[:], lhsT=wcodes[:, 0:P].bitcast(FP8X4), lhsT_scale=wscales[:, 0:P], rhs=wcodes[:].bitcast(FP8X4), rhs_scale=wscales[:], start=True, stop=True)
 
         def st_sums(i):
             st = chunks[i]
@@ -161,32 +161,22 @@ def tile_attngate_t_kernel(tc, q, k, attention_mask, cos, sin, wq, wk, out):
                     nc.scalar.copy(out=hi[:], in_=tp[:, :, 64:128])
                     st["tp"].append((c, half, tp, hi))
 
-        def st_tree_first(i):
+        def st_tree(i):
             st = chunks[i]
             groups = 16 if st["wide"] else 8
             first = work.tile([P, 2, groups, 64], BF16, name="first", tag="first%d" % groups)
             for c, half, tp, hi in st["tp"]:
                 nc.vector.tensor_tensor(out=first[:, c, half * 8:(half + 1) * 8, :], in0=tp[:, :, 0:64], in1=hi[:], op=ALU.max)
-            st["cur"] = first
-            st["width"] = 64
-
-        def st_tree_level(i):
-            st = chunks[i]
-            groups = 16 if st["wide"] else 8
-            if st["width"] == P // groups:
-                return
-            width = st["width"] // 2
-            cur = st["cur"]
-            nxt = work.tile([P, 2, groups, width], BF16, name="lvl", tag="lvl%d_%d" % (groups, width))
-            nc.vector.tensor_tensor(out=nxt[:], in0=cur[:, :, :, 0:width], in1=cur[:, :, :, width:2 * width], op=ALU.max)
-            st["cur"] = nxt
-            st["width"] = width
-
-        def st_regroup(i):
-            st = chunks[i]
+            cur = first
+            width = 64
+            while width > P // groups:
+                width = width // 2
+                nxt = work.tile([P, 2, groups, width], BF16, name="lvl", tag="lvl%d_%d" % (groups, width))
+                nc.vector.tensor_tensor(out=nxt[:], in0=cur[:, :, :, 0:width], in1=cur[:, :, :, width:2 * width], op=ALU.max)
+                cur = nxt
             grp = work.tile([P, P, 4], BF16, name="grp", tag="grp", align_bytes=64)
             nc.scalar.copy(out=grp[:, :, 0:2], in_=st["mean"][:].rearrange("p c b -> p b c"))
-            nc.scalar.copy(out=grp[:, :, 2:4], in_=st["cur"][:].rearrange("p c g b -> p (g b) c"))
+            nc.scalar.copy(out=grp[:, :, 2:4], in_=cur[:].rearrange("p c g b -> p (g b) c"))
             st["grp"] = grp
 
         def st_project(i):
@@ -196,28 +186,19 @@ def tile_attngate_t_kernel(tc, q, k, attention_mask, cos, sin, wq, wk, out):
             nc.vector.quantize_mx(out=pc[:].bitcast(FP8X4), scales=pscale[:], in_=st["grp"][:].rearrange("p b t -> p (b t)"))
             wcodes, wscales = weights[(st["kind"], st["h"])]
             xps = bank(1, [P, HID], F32, "xps")
+            fuel(xps, FUEL_P)
             nc.tensor.matmul_mx(out=xps[:], lhsT=pc[:].bitcast(FP8X4), lhsT_scale=pscale[:], rhs=wcodes[:].bitcast(FP8X4), rhs_scale=wscales[:], start=True, stop=True)
             st["xps"] = xps
 
-        def st_rope_a(i):
+        def st_rope(i):
             st = chunks[i]
-            if st["kind"] == "k":
-                nc.vector.tensor_scalar(out=nsin_sb[:, st["r"], :], in0=sin_sb[:, st["r"], 0:256], scalar1=-1.0, scalar2=None, op0=ALU.mult)
+            r = st["r"]
+            xps = st["xps"]
             m1 = work.tile([P, HID], F32, name="m1", tag="m1")
-            nc.vector.tensor_tensor(out=m1[:], in0=st["xps"][:], in1=cos_sb[:, st["r"], :], op=ALU.mult)
-            st["m1"] = m1
-
-        def st_rope_b(i):
-            st = chunks[i]
+            nc.vector.tensor_tensor(out=m1[:], in0=xps[:], in1=cos_sb[:, r, :], op=ALU.mult)
             m2 = work.tile([P, HID], F32, name="m2", tag="m2")
-            nc.vector.tensor_tensor(out=m2[:, 0:256], in0=st["xps"][:, 256:512], in1=nsin_sb[:, st["r"], :], op=ALU.mult)
-            st["m2"] = m2
-
-        def st_rope_c(i):
-            st = chunks[i]
-            m1 = st["m1"]
-            m2 = st["m2"]
-            nc.vector.tensor_tensor(out=m2[:, 256:512], in0=st["xps"][:, 0:256], in1=sin_sb[:, st["r"], 256:512], op=ALU.mult)
+            nc.vector.tensor_tensor(out=m2[:, 0:256], in0=xps[:, 256:512], in1=nsin_sb[:, r, :], op=ALU.mult)
+            nc.vector.tensor_tensor(out=m2[:, 256:512], in0=xps[:, 0:256], in1=sin_sb[:, r, 256:512], op=ALU.mult)
             if ROPE_ADD_ON_PE:
                 yt = bank(2, [P, 4, P], F32, "yt")
                 for t in range(4):
@@ -233,22 +214,23 @@ def tile_attngate_t_kernel(tc, q, k, attention_mask, cos, sin, wq, wk, out):
             nc.scalar.copy(out=g2[:], in_=yt[:].rearrange("p t b -> p b t"))
             st["g2"] = g2
 
-        def st_quant2(i):
+        def st_scores(i):
             st = chunks[i]
             r = st["r"]
             g2v = st["g2"][:].rearrange("p b t -> p (b t)")
             if st["kind"] == "k":
                 nc.vector.quantize_mx(out=kc[:, r * P:(r + 1) * P].bitcast(FP8X4), scales=ks[:, r * P:(r + 1) * P], in_=g2v)
-            else:
-                nc.vector.quantize_mx(out=qc_all[:, i - NR, :].bitcast(FP8X4), scales=qs_all[:, i - NR, :], in_=g2v)
-
-        def st_scores(i):
-            st = chunks[i]
+                return
+            qc = work.tile([P, P], U32, name="qc", tag="qc", align_bytes=64)
+            qs = work.tile([P, P], U8, name="qs", tag="qs", align_bytes=64)
+            nc.vector.quantize_mx(out=qc[:].bitcast(FP8X4), scales=qs[:], in_=g2v)
             st["sp"] = []
             for half in range(2):
                 cols = slice(half * 512, (half + 1) * 512)
                 sp = bank(5 + half, [P, 512], F32, "sp")
-                nc.tensor.matmul_mx(out=sp[:], lhsT=qc_all[:, i - NR, :].bitcast(FP8X4), lhsT_scale=qs_all[:, i - NR, :], rhs=kc[:, cols].bitcast(FP8X4), rhs_scale=ks[:, cols], start=True, stop=True)
+                if half == 0:
+                    fuel(sp, FUEL_S)
+                nc.tensor.matmul_mx(out=sp[:], lhsT=qc[:].bitcast(FP8X4), lhsT_scale=qs[:], rhs=kc[:, cols].bitcast(FP8X4), rhs_scale=ks[:, cols], start=True, stop=True)
                 st["sp"].append(sp)
 
         def st_mask(r):
@@ -256,28 +238,20 @@ def tile_attngate_t_kernel(tc, q, k, attention_mask, cos, sin, wq, wk, out):
             nc.scalar.activation(out=bias[:], in_=mask_tiles[r]["raw"][:].bitcast(U32).rearrange("p (w two) -> p w two", two=2)[:, :, 0], func=ACT.Copy, bias=-BIG, scale=BIG)
             mask_tiles[r]["bias"] = bias
 
-        def st_soft_add(i):
+        def st_softmax(i):
             st = chunks[i]
             bias = mask_tiles[st["r"]]["bias"]
-            t_sb = soft.tile([P, NB], F32, name="t_sb", tag="t_sb", bufs=3)
+            t_sb = soft.tile([P, NB], F32, name="t_sb", tag="t_sb")
             for half in range(2):
                 cols = slice(half * 512, (half + 1) * 512)
                 nc.vector.tensor_tensor(out=t_sb[:, cols], in0=st["sp"][half][:], in1=bias[:, cols], op=ALU.add)
-            st["t"] = t_sb
-
-        def st_soft_max(i):
-            st = chunks[i]
             mx = soft.tile([P, 1], F32, name="mx", tag="mx")
-            nc.vector.tensor_reduce(out=mx[:], in_=st["t"][:], axis=AX.X, op=ALU.max)
-            st["mx"] = mx
-
-        def st_soft_exp(i):
-            st = chunks[i]
+            nc.vector.tensor_reduce(out=mx[:], in_=t_sb[:], axis=AX.X, op=ALU.max)
             negm = soft.tile([P, 1], F32, name="negm", tag="negm")
-            nc.vector.tensor_scalar(out=negm[:], in0=st["mx"][:], scalar1=-SCALE, scalar2=None, op0=ALU.mult)
+            nc.vector.tensor_scalar(out=negm[:], in0=mx[:], scalar1=-SCALE, scalar2=None, op0=ALU.mult)
             e_sb = soft.tile([P, NB], F32, name="e_sb", tag="e_sb")
             ssum = soft.tile([P, 1], F32, name="ssum", tag="ssum")
-            nc.scalar.activation(out=e_sb[:], in_=st["t"][:], func=ACT.Exp, bias=negm[:], scale=SCALE, accum_out=ssum[:])
+            nc.scalar.activation(out=e_sb[:], in_=t_sb[:], func=ACT.Exp, bias=negm[:], scale=SCALE, accum_out=ssum[:])
             st["e"] = e_sb
             st["ssum"] = ssum
 
@@ -286,7 +260,7 @@ def tile_attngate_t_kernel(tc, q, k, attention_mask, cos, sin, wq, wk, out):
             rsum = soft.tile([P, 1], F32, name="rsum", tag="rsum")
             nc.vector.reciprocal(out=rsum[:], in_=st["ssum"][:])
             o_sb = soft.tile([P, NB], F32, name="o_sb", tag="o_sb", bufs=3)
-            if NORM == "gpsimd" and i < n_chunks - TAIL_V:
+            if NORM == "gpsimd":
                 nc.gpsimd.tensor_scalar(out=o_sb[:], in0=st["e"][:], scalar1=rsum[:], scalar2=0.0, op0=ALU.mult, op1=ALU.add)
             elif NORM == "scalar":
                 nc.scalar.activation(out=o_sb[:], in_=st["e"][:], func=ACT.Copy, scale=rsum[:])
@@ -297,10 +271,7 @@ def tile_attngate_t_kernel(tc, q, k, attention_mask, cos, sin, wq, wk, out):
         def st_store(i):
             st = chunks[i]
             r = st["r"]
-            if STORE == "gpsimd":
-                nc.gpsimd.dma_start(out=out[0, st["h"], r * P:(r + 1) * P, :], in_=st["o"][:])
-            else:
-                nc.sync.dma_start(out=out[0, st["h"], r * P:(r + 1) * P, :], in_=st["o"][:])
+            nc.sync.dma_start(out=out[0, st["h"], r * P:(r + 1) * P, :], in_=st["o"][:])
 
         def is_q(i):
             return 0 <= i < n_chunks and chunks[i]["kind"] == "q"
@@ -309,56 +280,40 @@ def tile_attngate_t_kernel(tc, q, k, attention_mask, cos, sin, wq, wk, out):
             return 0 <= i < n_chunks
 
         raws = {}
-        for n in range(n_chunks + 9 + LEAD):
-            s = n - LEAD
+        for n in range(n_chunks + 8):
+            if is_q(n - 6):
+                st_norm(n - 6)
+            if is_q(n - 7):
+                st_store(n - 7)
+            if valid(n - 1):
+                st_transpose(n - 1)
             if valid(n + PF):
                 load_chunk(n + PF)
-            if n == 0:
+            if n == 2:
                 raws[0] = load_weight(wq[0], "q0")
-            if n == 1:
+            if n == 3:
                 raws[1] = load_weight(wq[1], "q1")
-            if is_q(s + 1) and chunks[s + 1]["h"] == 0:
-                load_mask(chunks[s + 1]["r"])
             if valid(n):
                 st_sums(n)
-                st_l1(n)
             if n == 0:
                 weights[("k", 0)] = prep_weight(raw_k, "k")
-            if is_q(s - 2) and chunks[s - 2]["h"] == 0:
-                st_mask(chunks[s - 2]["r"])
-            if is_q(s - 5):
-                st_soft_add(s - 5)
-            if is_q(s - 4):
-                st_scores(s - 4)
-            if valid(n - 1):
-                st_tree_first(n - 1)
-            if valid(n):
-                st_transpose(n)
-            if is_q(s - 6):
-                st_soft_max(s - 6)
-            if valid(n - 3):
-                st_rope_a(n - 3)
-            if is_q(s - 7):
-                st_norm(s - 7)
-                st_store(s - 7)
-            if valid(n - 1):
-                st_tree_level(n - 1)
-            if is_q(s - 6):
-                st_soft_exp(s - 6)
-            if valid(n - 3):
-                st_rope_b(n - 3)
-            if valid(n - 1):
-                st_tree_level(n - 1)
-            if valid(n - 3):
-                st_rope_c(n - 3)
-            if n == 3:
+            if n == 5:
                 weights[("q", 0)] = prep_weight(raws[0], "q0")
-            if n == 4:
+            if n == 6:
                 weights[("q", 1)] = prep_weight(raws[1], "q1")
+            if is_q(n - 2) and chunks[n - 2]["h"] == 0:
+                st_mask(chunks[n - 2]["r"])
+            if is_q(n - 5):
+                st_softmax(n - 5)
+            if valid(n - 3):
+                st_rope(n - 3)
             if valid(n - 1):
-                st_tree_level(n - 1)
-                st_regroup(n - 1)
+                st_tree(n - 1)
+            if n == 2:
+                nc.vector.tensor_scalar(out=nsin_sb[:], in0=sin_sb[:, :, 0:256], scalar1=-1.0, scalar2=None, op0=ALU.mult)
             if valid(n - 2):
                 st_project(n - 2)
             if valid(n - 4):
-                st_quant2(n - 4)
+                st_scores(n - 4)
+            if valid(n):
+                st_l1(n)

@@ -30,6 +30,7 @@ ROPE_ADD_ON_PE = True
 NORM = "gpsimd"
 WIDE_K = (0, 1, 2, 3)
 PF = 3
+RUNS = 4
 FUEL_S = 2
 FUEL_P = 2
 
@@ -60,9 +61,13 @@ def tile_attngate_t_kernel(tc, q, k, attention_mask, cos, sin, wq, wk, out):
             rows = st["src"][r * CHUNK:(r + 1) * CHUNK, :]
             x = xin.tile([P, 4096], BF16, name="x", tag="x")
             if st["wide"]:
-                nc.sync.dma_start(out=x[:].rearrange("p (g d) -> p g d", g=16), in_=rows.rearrange("(g p) d -> p g d", g=16, p=P))
+                xv = x[:].rearrange("p (g d) -> p g d", g=16)
+                rv = rows.rearrange("(g p) d -> p g d", g=16, p=P)
             else:
-                nc.sync.dma_start(out=x[:].rearrange("p (g e) -> p g e", g=8), in_=rows.rearrange("(g p l) d -> p g (l d)", g=8, p=P, l=2))
+                xv = x[:].rearrange("p (g e) -> p g e", g=8)
+                rv = rows.rearrange("(g p l) d -> p g (l d)", g=8, p=P, l=2)
+            for g0 in range(0, xv.shape[1], RUNS):
+                nc.sync.dma_start(out=xv[:, g0:g0 + RUNS, :], in_=rv[:, g0:g0 + RUNS, :])
             st["x"] = x
             if st["kind"] == "q" and st["h"] == 0:
                 mraw = soft.tile([P, 2 * NB], I32, name="mraw", tag="mraw", bufs=3)
@@ -86,9 +91,11 @@ def tile_attngate_t_kernel(tc, q, k, attention_mask, cos, sin, wq, wk, out):
         raw_k = load_weight(wk[0], "k")
         load_chunk(1)
         cos_sb = const.tile([P, NR, HID], BF16, name="cos_sb")
-        nc.sync.dma_start(out=cos_sb[:], in_=cos[0].rearrange("(r p) h -> p r h", p=P))
+        for r0 in range(0, NR, RUNS):
+            nc.sync.dma_start(out=cos_sb[:, r0:r0 + RUNS, :], in_=cos[0].rearrange("(r p) h -> p r h", p=P)[:, r0:r0 + RUNS, :])
         sin_sb = const.tile([P, NR, HID], BF16, name="sin_sb")
-        nc.sync.dma_start(out=sin_sb[:], in_=sin[0].rearrange("(r p) h -> p r h", p=P))
+        for r0 in range(0, NR, RUNS):
+            nc.sync.dma_start(out=sin_sb[:, r0:r0 + RUNS, :], in_=sin[0].rearrange("(r p) h -> p r h", p=P)[:, r0:r0 + RUNS, :])
         load_chunk(2)
 
         ident = const.tile([P, P], BF16, name="ident")

@@ -27,10 +27,9 @@ FLOPS = 2 * 3 * NB * HID * HID + 2 * 2 * NB * NB * HID
 
 PIN = False
 ROPE_ADD_ON_PE = True
-NORM = "gpsimd"
+NORM = "scalar"
 WIDE_K = (0, 1, 2, 3)
 PF = 3
-RUNS = 4
 FUEL_S = 2
 FUEL_P = 2
 
@@ -61,13 +60,9 @@ def tile_attngate_t_kernel(tc, q, k, attention_mask, cos, sin, wq, wk, out):
             rows = st["src"][r * CHUNK:(r + 1) * CHUNK, :]
             x = xin.tile([P, 4096], BF16, name="x", tag="x")
             if st["wide"]:
-                xv = x[:].rearrange("p (g d) -> p g d", g=16)
-                rv = rows.rearrange("(g p) d -> p g d", g=16, p=P)
+                nc.sync.dma_start(out=x[:].rearrange("p (g d) -> p g d", g=16), in_=rows.rearrange("(g p) d -> p g d", g=16, p=P))
             else:
-                xv = x[:].rearrange("p (g e) -> p g e", g=8)
-                rv = rows.rearrange("(g p l) d -> p g (l d)", g=8, p=P, l=2)
-            for g0 in range(0, xv.shape[1], RUNS):
-                nc.sync.dma_start(out=xv[:, g0:g0 + RUNS, :], in_=rv[:, g0:g0 + RUNS, :])
+                nc.sync.dma_start(out=x[:].rearrange("p (g e) -> p g e", g=8), in_=rows.rearrange("(g p l) d -> p g (l d)", g=8, p=P, l=2))
             st["x"] = x
             if st["kind"] == "q" and st["h"] == 0:
                 mraw = soft.tile([P, 2 * NB], I32, name="mraw", tag="mraw", bufs=3)
@@ -91,11 +86,9 @@ def tile_attngate_t_kernel(tc, q, k, attention_mask, cos, sin, wq, wk, out):
         raw_k = load_weight(wk[0], "k")
         load_chunk(1)
         cos_sb = const.tile([P, NR, HID], BF16, name="cos_sb")
-        for r0 in range(0, NR, RUNS):
-            nc.sync.dma_start(out=cos_sb[:, r0:r0 + RUNS, :], in_=cos[0].rearrange("(r p) h -> p r h", p=P)[:, r0:r0 + RUNS, :])
+        nc.sync.dma_start(out=cos_sb[:], in_=cos[0].rearrange("(r p) h -> p r h", p=P))
         sin_sb = const.tile([P, NR, HID], BF16, name="sin_sb")
-        for r0 in range(0, NR, RUNS):
-            nc.sync.dma_start(out=sin_sb[:, r0:r0 + RUNS, :], in_=sin[0].rearrange("(r p) h -> p r h", p=P)[:, r0:r0 + RUNS, :])
+        nc.sync.dma_start(out=sin_sb[:], in_=sin[0].rearrange("(r p) h -> p r h", p=P))
         load_chunk(2)
 
         ident = const.tile([P, P], BF16, name="ident")
@@ -158,15 +151,16 @@ def tile_attngate_t_kernel(tc, q, k, attention_mask, cos, sin, wq, wk, out):
             perm = perm16 if st["wide"] else perm8
             src = st["tsrc"]
             st["tp"] = []
-            for c in range(2):
-                for half in range(halves):
-                    j = c * halves + half
-                    tp = bank(3 + j, [P, 8, P], BF16, "tp")
-                    for g in range(8):
-                        nc.tensor.transpose(out=tp[:, g, :], in_=src[:, half * 8 + g, c * P:(c + 1) * P], identity=perm[:])
-                    hi = work.tile([P, 8, 64], BF16, name="hi", tag="hi%d" % j)
-                    nc.scalar.copy(out=hi[:], in_=tp[:, :, 64:128])
-                    st["tp"].append((c, half, tp, hi))
+            for half in range(halves):
+                tps = [bank(3 + c * halves + half, [P, 8, P], BF16, "tp") for c in range(2)]
+                for quad in range(2):
+                    for c in range(2):
+                        for g in range(quad * 4, quad * 4 + 4):
+                            nc.tensor.transpose(out=tps[c][:, g, :], in_=src[:, half * 8 + g, c * P:(c + 1) * P], identity=perm[:])
+                for c in range(2):
+                    hi = work.tile([P, 8, 64], BF16, name="hi", tag="hi%d" % (c * halves + half))
+                    nc.scalar.copy(out=hi[:], in_=tps[c][:, :, 64:128])
+                    st["tp"].append((c, half, tps[c], hi))
 
         def st_tree(i):
             st = chunks[i]
@@ -278,7 +272,10 @@ def tile_attngate_t_kernel(tc, q, k, attention_mask, cos, sin, wq, wk, out):
         def st_store(i):
             st = chunks[i]
             r = st["r"]
-            nc.sync.dma_start(out=out[0, st["h"], r * P:(r + 1) * P, :], in_=st["o"][:])
+            if NORM == "scalar":
+                nc.scalar.dma_start(out=out[0, st["h"], r * P:(r + 1) * P, :], in_=st["o"][:])
+            else:
+                nc.sync.dma_start(out=out[0, st["h"], r * P:(r + 1) * P, :], in_=st["o"][:])
 
         def is_q(i):
             return 0 <= i < n_chunks and chunks[i]["kind"] == "q"

@@ -27,7 +27,7 @@ FLOPS = 2 * 3 * NB * HID * HID + 2 * 2 * NB * NB * HID
 
 PIN = False
 ROPE_ADD_ON_PE = True
-NORM = "scalar"
+NORM = "gpsimd"
 WIDE_K = (0, 1, 2, 3)
 PF = 3
 FUEL_S = 2
@@ -39,7 +39,7 @@ def tile_attngate_t_kernel(tc, q, k, attention_mask, cos, sin, wq, wk, out):
     with ExitStack() as ctx:
         const = ctx.enter_context(tc.tile_pool(name="const", bufs=1))
         xin = ctx.enter_context(tc.tile_pool(name="xin", bufs=PF + 3))
-        work = ctx.enter_context(tc.tile_pool(name="work", bufs=2))
+        work = ctx.enter_context(tc.tile_pool(name="work", bufs=3))
         soft = ctx.enter_context(tc.tile_pool(name="soft", bufs=2))
         psum = ctx.enter_context(tc.psum_pool(name="psum", bufs=1))
         if PIN:
@@ -76,7 +76,7 @@ def tile_attngate_t_kernel(tc, q, k, attention_mask, cos, sin, wq, wk, out):
 
         def prep_weight(raw, name):
             grouped = const.tile([P, HID, 4], BF16, name="grp_" + name, tag="wgrp", align_bytes=64)
-            nc.vector.tensor_copy(out=grouped[:], in_=raw[:].rearrange("p t n -> p n t"))
+            nc.scalar.copy(out=grouped[:], in_=raw[:].rearrange("p t n -> p n t"))
             codes = const.tile([P, HID], U32, name="wc_" + name, align_bytes=64)
             scales = const.tile([P, HID], U8, name="ws_" + name, align_bytes=64)
             nc.vector.quantize_mx(out=codes[:].bitcast(FP8X4), scales=scales[:], in_=grouped[:].rearrange("p n t -> p (n t)"))
@@ -151,28 +151,27 @@ def tile_attngate_t_kernel(tc, q, k, attention_mask, cos, sin, wq, wk, out):
             perm = perm16 if st["wide"] else perm8
             src = st["tsrc"]
             st["tp"] = []
-            for half in range(halves):
-                tps = [bank(3 + c * halves + half, [P, 8, P], BF16, "tp") for c in range(2)]
-                for quad in range(2):
-                    for c in range(2):
-                        for g in range(quad * 4, quad * 4 + 4):
-                            nc.tensor.transpose(out=tps[c][:, g, :], in_=src[:, half * 8 + g, c * P:(c + 1) * P], identity=perm[:])
-                for c in range(2):
-                    hi = work.tile([P, 8, 64], BF16, name="hi", tag="hi%d" % (c * halves + half))
-                    nc.scalar.copy(out=hi[:], in_=tps[c][:, :, 64:128])
-                    st["tp"].append((c, half, tps[c], hi))
+            for c in range(2):
+                for half in range(halves):
+                    j = c * halves + half
+                    tp = bank(3 + j, [P, 8, P], BF16, "tp")
+                    for g in range(8):
+                        nc.tensor.transpose(out=tp[:, g, :], in_=src[:, half * 8 + g, c * P:(c + 1) * P], identity=perm[:])
+                    hi = work.tile([P, 8, 64], BF16, name="hi", tag="hi%d" % j)
+                    nc.scalar.copy(out=hi[:], in_=tp[:, :, 64:128])
+                    st["tp"].append((c, half, tp, hi))
 
         def st_tree(i):
             st = chunks[i]
             groups = 16 if st["wide"] else 8
-            first = work.tile([P, 2, groups, 64], BF16, name="first", tag="first%d" % groups)
+            first = work.tile([P, 2, groups, 64], BF16, name="first", tag="first%d" % groups, bufs=2)
             for c, half, tp, hi in st["tp"]:
                 nc.vector.tensor_tensor(out=first[:, c, half * 8:(half + 1) * 8, :], in0=tp[:, :, 0:64], in1=hi[:], op=ALU.max)
             cur = first
             width = 64
             while width > P // groups:
                 width = width // 2
-                nxt = work.tile([P, 2, groups, width], BF16, name="lvl", tag="lvl%d_%d" % (groups, width))
+                nxt = work.tile([P, 2, groups, width], BF16, name="lvl", tag="lvl%d_%d" % (groups, width), bufs=2)
                 nc.vector.tensor_tensor(out=nxt[:], in0=cur[:, :, :, 0:width], in1=cur[:, :, :, width:2 * width], op=ALU.max)
                 cur = nxt
             grp = work.tile([P, P, 4], BF16, name="grp", tag="grp", align_bytes=64)
@@ -245,14 +244,12 @@ def tile_attngate_t_kernel(tc, q, k, attention_mask, cos, sin, wq, wk, out):
             t_sb = soft.tile([P, NB], F32, name="t_sb", tag="t_sb")
             for half in range(2):
                 cols = slice(half * 512, (half + 1) * 512)
-                nc.vector.tensor_tensor(out=t_sb[:, cols], in0=st["sp"][half][:], in1=bias[:, cols], op=ALU.add)
-            mx = soft.tile([P, 1], F32, name="mx", tag="mx")
-            nc.vector.tensor_reduce(out=mx[:], in_=t_sb[:], axis=AX.X, op=ALU.max)
+                nc.vector.scalar_tensor_tensor(out=t_sb[:, cols], in0=st["sp"][half][:], scalar=SCALE, in1=bias[:, cols], op0=ALU.mult, op1=ALU.add)
             negm = soft.tile([P, 1], F32, name="negm", tag="negm")
-            nc.vector.tensor_scalar(out=negm[:], in0=mx[:], scalar1=-SCALE, scalar2=None, op0=ALU.mult)
+            nc.vector.tensor_reduce(out=negm[:], in_=t_sb[:], axis=AX.X, op=ALU.max, negate=True)
             e_sb = soft.tile([P, NB], F32, name="e_sb", tag="e_sb")
             ssum = soft.tile([P, 1], F32, name="ssum", tag="ssum")
-            nc.scalar.activation(out=e_sb[:], in_=t_sb[:], func=ACT.Exp, bias=negm[:], scale=SCALE, accum_out=ssum[:])
+            nc.scalar.activation(out=e_sb[:], in_=t_sb[:], func=ACT.Exp, bias=negm[:], scale=1.0, accum_out=ssum[:])
             st["e"] = e_sb
             st["ssum"] = ssum
 
@@ -261,7 +258,7 @@ def tile_attngate_t_kernel(tc, q, k, attention_mask, cos, sin, wq, wk, out):
             rsum = soft.tile([P, 1], F32, name="rsum", tag="rsum")
             nc.vector.reciprocal(out=rsum[:], in_=st["ssum"][:])
             o_sb = soft.tile([P, NB], F32, name="o_sb", tag="o_sb", bufs=3)
-            if NORM == "gpsimd":
+            if NORM == "gpsimd" and i < n_chunks - 2:
                 nc.gpsimd.tensor_scalar(out=o_sb[:], in0=st["e"][:], scalar1=rsum[:], scalar2=0.0, op0=ALU.mult, op1=ALU.add)
             elif NORM == "scalar":
                 nc.scalar.activation(out=o_sb[:], in_=st["e"][:], func=ACT.Copy, scale=rsum[:])
@@ -272,10 +269,7 @@ def tile_attngate_t_kernel(tc, q, k, attention_mask, cos, sin, wq, wk, out):
         def st_store(i):
             st = chunks[i]
             r = st["r"]
-            if NORM == "scalar":
-                nc.scalar.dma_start(out=out[0, st["h"], r * P:(r + 1) * P, :], in_=st["o"][:])
-            else:
-                nc.sync.dma_start(out=out[0, st["h"], r * P:(r + 1) * P, :], in_=st["o"][:])
+            nc.sync.dma_start(out=out[0, st["h"], r * P:(r + 1) * P, :], in_=st["o"][:])
 
         def is_q(i):
             return 0 <= i < n_chunks and chunks[i]["kind"] == "q"

@@ -25,9 +25,6 @@ BIG = 2.0 ** 35
 
 FLOPS = 2 * 3 * NB * HID * HID + 2 * 2 * NB * NB * HID
 
-PIN = False
-ROPE_ADD_ON_PE = True
-NORM = "gpsimd"
 WIDE_K = (0, 1, 2, 3)
 PF = 3
 FUEL_S = 2
@@ -42,8 +39,6 @@ def tile_attngate_t_kernel(tc, q, k, attention_mask, cos, sin, wq, wk, out):
         work = ctx.enter_context(tc.tile_pool(name="work", bufs=3))
         soft = ctx.enter_context(tc.tile_pool(name="soft", bufs=2))
         psum = ctx.enter_context(tc.psum_pool(name="psum", bufs=1))
-        if PIN:
-            ctx.enter_context(tc.manual_schedule())
 
         chunks = [{"kind": "k", "h": 0, "r": r, "wide": r in WIDE_K, "src": k[0, 0]} for r in range(NR)]
         chunks.extend([{"kind": "q", "h": h, "r": r, "wide": False, "src": q[0, h]} for r in range(NR) for h in range(2)])
@@ -85,10 +80,10 @@ def tile_attngate_t_kernel(tc, q, k, attention_mask, cos, sin, wq, wk, out):
         load_chunk(0)
         raw_k = load_weight(wk[0], "k")
         load_chunk(1)
-        cos_sb = const.tile([P, NR, HID], BF16, name="cos_sb")
-        nc.sync.dma_start(out=cos_sb[:], in_=cos[0].rearrange("(r p) h -> p r h", p=P))
-        sin_sb = const.tile([P, NR, HID], BF16, name="sin_sb")
-        nc.sync.dma_start(out=sin_sb[:], in_=sin[0].rearrange("(r p) h -> p r h", p=P))
+        tab = const.tile([P, NR, 2, HID], BF16, name="tab")
+        nc.sync.dma_start(out=tab[:, :, 0, :], in_=cos[0].rearrange("(r p) h -> p r h", p=P))
+        nc.sync.dma_start(out=tab[:, :, 1, 0:256], in_=sin[0, :, 256:512].rearrange("(r p) h -> p r h", p=P))
+        nc.sync.dma_start(out=tab[:, :, 1, 256:512], in_=sin[0, :, 0:256].rearrange("(r p) h -> p r h", p=P))
         load_chunk(2)
 
         ident = const.tile([P, P], BF16, name="ident")
@@ -111,7 +106,6 @@ def tile_attngate_t_kernel(tc, q, k, attention_mask, cos, sin, wq, wk, out):
         kc = const.tile([P, NB], U32, name="kc", align_bytes=64)
         ks = const.tile([P, NB], U8, name="ks", align_bytes=64)
         weights = {}
-        nsin_sb = const.tile([P, NR, 256], BF16, name="nsin_sb")
 
         def fuel(target, count):
             wcodes, wscales = weights[("k", 0)]
@@ -194,22 +188,13 @@ def tile_attngate_t_kernel(tc, q, k, attention_mask, cos, sin, wq, wk, out):
             st = chunks[i]
             r = st["r"]
             xps = st["xps"]
-            m1 = work.tile([P, HID], F32, name="m1", tag="m1")
-            nc.vector.tensor_tensor(out=m1[:], in0=xps[:], in1=cos_sb[:, r, :], op=ALU.mult)
-            m2 = work.tile([P, HID], F32, name="m2", tag="m2")
-            nc.vector.tensor_tensor(out=m2[:, 0:256], in0=xps[:, 256:512], in1=nsin_sb[:, r, :], op=ALU.mult)
-            nc.vector.tensor_tensor(out=m2[:, 256:512], in0=xps[:, 0:256], in1=sin_sb[:, r, 256:512], op=ALU.mult)
-            if ROPE_ADD_ON_PE:
-                yt = bank(2, [P, 4, P], F32, "yt")
-                for t in range(4):
-                    nc.tensor.matmul(out=yt[:, t, :], lhsT=m1[:, t * P:(t + 1) * P], rhs=identf[:], is_transpose=True, start=True, stop=False)
-                    nc.tensor.matmul(out=yt[:, t, :], lhsT=m2[:, t * P:(t + 1) * P], rhs=identf[:], is_transpose=True, start=False, stop=True)
-            else:
-                y = work.tile([P, HID], BF16, name="y", tag="y")
-                nc.vector.tensor_tensor(out=y[:], in0=m1[:], in1=m2[:], op=ALU.add)
-                yt = bank(2, [P, 4, P], BF16, "yt")
-                for t in range(4):
-                    nc.tensor.transpose(out=yt[:, t, :], in_=y[:, t * P:(t + 1) * P], identity=ident[:])
+            m = work.tile([P, 2, HID], F32, name="m", tag="m")
+            nc.vector.tensor_tensor(out=m[:], in0=xps[:].unsqueeze(1).to_broadcast([P, 2, HID]), in1=tab[:, r], op=ALU.mult)
+            yt = bank(2, [P, 4, P], F32, "yt")
+            for t in range(4):
+                u = t ^ 2
+                nc.tensor.matmul(out=yt[:, t, :], lhsT=m[:, 0, t * P:(t + 1) * P], rhs=identf[:], is_transpose=True, start=True, stop=False)
+                nc.tensor.matmul(out=yt[:, t, :], lhsT=m[:, 1, u * P:(u + 1) * P], rhs=identf[:], is_transpose=True, start=False, stop=True)
             g2 = work.tile([P, P, 4], BF16, name="g2", tag="g2", align_bytes=64)
             nc.scalar.copy(out=g2[:], in_=yt[:].rearrange("p t b -> p b t"))
             st["g2"] = g2
@@ -258,9 +243,7 @@ def tile_attngate_t_kernel(tc, q, k, attention_mask, cos, sin, wq, wk, out):
             rsum = soft.tile([P, 1], F32, name="rsum", tag="rsum")
             nc.vector.reciprocal(out=rsum[:], in_=st["ssum"][:])
             o_sb = soft.tile([P, NB], F32, name="o_sb", tag="o_sb", bufs=3)
-            if NORM == "gpsimd" and i < n_chunks - 2:
-                nc.gpsimd.tensor_scalar(out=o_sb[:], in0=st["e"][:], scalar1=rsum[:], scalar2=0.0, op0=ALU.mult, op1=ALU.add)
-            elif NORM == "scalar":
+            if i < n_chunks - 2:
                 nc.scalar.activation(out=o_sb[:], in_=st["e"][:], func=ACT.Copy, scale=rsum[:])
             else:
                 nc.vector.tensor_scalar(out=o_sb[:], in0=st["e"][:], scalar1=rsum[:], scalar2=None, op0=ALU.mult)
@@ -308,7 +291,7 @@ def tile_attngate_t_kernel(tc, q, k, attention_mask, cos, sin, wq, wk, out):
             if valid(n - 1):
                 st_tree(n - 1)
             if n == 2:
-                nc.vector.tensor_scalar(out=nsin_sb[:], in0=sin_sb[:, :, 0:256], scalar1=-1.0, scalar2=None, op0=ALU.mult)
+                nc.vector.tensor_scalar(out=tab[:, :, 1, 256:512], in0=tab[:, :, 1, 256:512], scalar1=-1.0, scalar2=None, op0=ALU.mult)
             if valid(n - 2):
                 st_project(n - 2)
             if valid(n - 4):

@@ -27,8 +27,8 @@ FLOPS = 2 * 3 * NB * HID * HID + 2 * 2 * NB * NB * HID
 
 WIDE_K = (0, 1, 2, 3)
 PF = 3
-FUEL_S = 2
-FUEL_P = 2
+FUEL_S = 1
+FUEL_P = 1
 
 
 def tile_attngate_t_kernel(tc, q, k, attention_mask, cos, sin, wq, wk, out):
@@ -152,7 +152,7 @@ def tile_attngate_t_kernel(tc, q, k, attention_mask, cos, sin, wq, wk, out):
                     for g in range(8):
                         nc.tensor.transpose(out=tp[:, g, :], in_=src[:, half * 8 + g, c * P:(c + 1) * P], identity=perm[:])
                     hi = work.tile([P, 8, 64], BF16, name="hi", tag="hi%d" % j)
-                    nc.scalar.copy(out=hi[:], in_=tp[:, :, 64:128])
+                    nc.scalar.copy(out=hi[:].rearrange("p g b -> p (g b)").bitcast(F32).rearrange("p (g b) -> p g b", g=8), in_=tp[:].rearrange("p g b -> p (g b)").bitcast(F32).rearrange("p (g b) -> p g b", g=8)[:, :, 32:64])
                     st["tp"].append((c, half, tp, hi))
 
         def st_tree(i):
@@ -188,13 +188,24 @@ def tile_attngate_t_kernel(tc, q, k, attention_mask, cos, sin, wq, wk, out):
             st = chunks[i]
             r = st["r"]
             xps = st["xps"]
-            m = work.tile([P, 2, HID], F32, name="m", tag="m")
-            nc.vector.tensor_tensor(out=m[:], in0=xps[:].unsqueeze(1).to_broadcast([P, 2, HID]), in1=tab[:, r], op=ALU.mult)
+            m1 = work.tile([P, HID], F32, name="m1", tag="m1")
+            m2 = work.tile([P, HID], F32, name="m2", tag="m2")
+            xc = work.tile([P, HID], F32, name="xc", tag="xc")
+            nc.scalar.copy(out=xc[:], in_=xps[:])
+            for half in range(2):
+                hs = slice(half * 256, (half + 1) * 256)
+                nc.gpsimd.tensor_tensor(out=m2[:, hs], in0=xc[:, hs], in1=tab[:, r, 1, hs], op=ALU.mult)
+            nc.vector.tensor_tensor(out=m1[:], in0=xps[:], in1=tab[:, r, 0, :], op=ALU.mult)
+            st["m"] = (m1, m2)
+
+        def st_rope_turn(i):
+            st = chunks[i]
+            m1, m2 = st["m"]
             yt = bank(2, [P, 4, P], F32, "yt")
             for t in range(4):
                 u = t ^ 2
-                nc.tensor.matmul(out=yt[:, t, :], lhsT=m[:, 0, t * P:(t + 1) * P], rhs=identf[:], is_transpose=True, start=True, stop=False)
-                nc.tensor.matmul(out=yt[:, t, :], lhsT=m[:, 1, u * P:(u + 1) * P], rhs=identf[:], is_transpose=True, start=False, stop=True)
+                nc.tensor.matmul(out=yt[:, t, :], lhsT=m1[:, t * P:(t + 1) * P], rhs=identf[:], is_transpose=True, start=True, stop=False)
+                nc.tensor.matmul(out=yt[:, t, :], lhsT=m2[:, u * P:(u + 1) * P], rhs=identf[:], is_transpose=True, start=False, stop=True)
             g2 = work.tile([P, P, 4], BF16, name="g2", tag="g2", align_bytes=64)
             nc.scalar.copy(out=g2[:], in_=yt[:].rearrange("p t b -> p b t"))
             st["g2"] = g2
@@ -261,11 +272,11 @@ def tile_attngate_t_kernel(tc, q, k, attention_mask, cos, sin, wq, wk, out):
             return 0 <= i < n_chunks
 
         raws = {}
-        for n in range(n_chunks + 8):
-            if is_q(n - 6):
-                st_norm(n - 6)
+        for n in range(n_chunks + 9):
             if is_q(n - 7):
-                st_store(n - 7)
+                st_norm(n - 7)
+            if is_q(n - 8):
+                st_store(n - 8)
             if valid(n - 1):
                 st_transpose(n - 1)
             if valid(n + PF):
@@ -284,8 +295,10 @@ def tile_attngate_t_kernel(tc, q, k, attention_mask, cos, sin, wq, wk, out):
                 weights[("q", 1)] = prep_weight(raws[1], "q1")
             if is_q(n - 2) and chunks[n - 2]["h"] == 0:
                 st_mask(chunks[n - 2]["r"])
-            if is_q(n - 5):
-                st_softmax(n - 5)
+            if is_q(n - 6):
+                st_softmax(n - 6)
+            if valid(n - 4):
+                st_rope_turn(n - 4)
             if valid(n - 3):
                 st_rope(n - 3)
             if valid(n - 1):
@@ -294,7 +307,7 @@ def tile_attngate_t_kernel(tc, q, k, attention_mask, cos, sin, wq, wk, out):
                 nc.vector.tensor_scalar(out=tab[:, :, 1, 256:512], in0=tab[:, :, 1, 256:512], scalar1=-1.0, scalar2=None, op0=ALU.mult)
             if valid(n - 2):
                 st_project(n - 2)
-            if valid(n - 4):
-                st_scores(n - 4)
+            if valid(n - 5):
+                st_scores(n - 5)
             if valid(n):
                 st_l1(n)

from contextlib import ExitStack
import math

import concourse.mybir as mybir
from concourse.masks import make_identity

BF16 = mybir.dt.bfloat16
F32 = mybir.dt.float32
I32 = mybir.dt.int32
U32 = mybir.dt.uint32
U8 = mybir.dt.uint8
FP8X4 = mybir.dt.float8_e4m3fn_x4
ALU = mybir.AluOpType
ACT = mybir.ActivationFunctionType
AX = mybir.AxisListType

P = 128
D = 256
HID = 512
NB = 1024
CHUNK = 2048
NR = 8
SCALE = 1.0 / math.sqrt(512.0)
BIG = 2.0 ** 35

FLOPS = 2 * 3 * NB * HID * HID + 2 * 2 * NB * NB * HID

WIDE_K = (0, 1, 2, 3)
PF = 3
FUEL_S = 1
FUEL_P = 1


def tile_attngate_t_kernel(tc, q, k, attention_mask, cos, sin, wq, wk, out):
    nc = tc.nc
    with ExitStack() as ctx:
        const = ctx.enter_context(tc.tile_pool(name="const", bufs=1))
        xin = ctx.enter_context(tc.tile_pool(name="xin", bufs=PF + 3))
        work = ctx.enter_context(tc.tile_pool(name="work", bufs=3))
        soft = ctx.enter_context(tc.tile_pool(name="soft", bufs=2))
        psum = ctx.enter_context(tc.psum_pool(name="psum", bufs=1))

        chunks = [{"kind": "k", "h": 0, "r": r, "wide": r in WIDE_K, "src": k[0, 0]} for r in range(NR)]
        chunks.extend([{"kind": "q", "h": h, "r": r, "wide": False, "src": q[0, h]} for r in range(NR) for h in range(2)])
        n_chunks = len(chunks)
        mask32 = attention_mask[0, 0].bitcast(I32).rearrange("(r p) w -> r p w", p=P)
        mask_tiles = {}

        def bank(i, shape, dtype, name):
            return psum.tile(shape, dtype, name=name, tag="bank%d" % i)

        def load_chunk(i):
            st = chunks[i]
            r = st["r"]
            rows = st["src"][r * CHUNK:(r + 1) * CHUNK, :]
            x = xin.tile([P, 4096], BF16, name="x", tag="x")
            if st["wide"]:
                nc.sync.dma_start(out=x[:].rearrange("p (g d) -> p g d", g=16), in_=rows.rearrange("(g p) d -> p g d", g=16, p=P))
            else:
                nc.sync.dma_start(out=x[:].rearrange("p (g e) -> p g e", g=8), in_=rows.rearrange("(g p l) d -> p g (l d)", g=8, p=P, l=2))
            st["x"] = x
            if st["kind"] == "q" and st["h"] == 0:
                mraw = soft.tile([P, 2 * NB], I32, name="mraw", tag="mraw", bufs=3)
                nc.sync.dma_start(out=mraw[:], in_=mask32[r])
                mask_tiles[r] = {"raw": mraw}

        def load_weight(w, name):
            raw = const.tile([P, 4, HID], BF16, name="raw_" + name, tag="wraw", bufs=2)
            nc.sync.dma_start(out=raw[:], in_=w.rearrange("(t p) n -> p t n", t=4, p=P))
            return raw

        def prep_weight(raw, name):
            grouped = const.tile([P, HID, 4], BF16, name="grp_" + name, tag="wgrp", align_bytes=64)
            nc.scalar.copy(out=grouped[:], in_=raw[:].rearrange("p t n -> p n t"))
            codes = const.tile([P, HID], U32, name="wc_" + name, align_bytes=64)
            scales = const.tile([P, HID], U8, name="ws_" + name, align_bytes=64)
            nc.vector.quantize_mx(out=codes[:].bitcast(FP8X4), scales=scales[:], in_=grouped[:].rearrange("p n t -> p (n t)"))
            return codes, scales

        load_chunk(0)
        raw_k = load_weight(wk[0], "k")
        load_chunk(1)
        tab = const.tile([P, NR, 2, HID], BF16, name="tab")
        nc.sync.dma_start(out=tab[:, :, 0, :], in_=cos[0].rearrange("(r p) h -> p r h", p=P))
        nc.sync.dma_start(out=tab[:, :, 1, 0:256], in_=sin[0, :, 256:512].rearrange("(r p) h -> p r h", p=P))
        nc.sync.dma_start(out=tab[:, :, 1, 256:512], in_=sin[0, :, 0:256].rearrange("(r p) h -> p r h", p=P))
        load_chunk(2)

        ident = const.tile([P, P], BF16, name="ident")
        make_identity(nc, ident[:])
        identf = const.tile([P, P], F32, name="identf")
        make_identity(nc, identf[:])
        perm8 = const.tile([P, P], BF16, name="perm8")
        nc.vector.tensor_copy(out=perm8[:].rearrange("p (h b) -> p h b", h=8), in_=ident[:].rearrange("p (b h) -> p h b", h=8))
        perm16 = const.tile([P, P], BF16, name="perm16")
        nc.vector.tensor_copy(out=perm16[:].rearrange("p (h b) -> p h b", h=16), in_=ident[:].rearrange("p (b h) -> p h b", h=16))
        cnt8 = const.tile([P, 16], F32, name="cnt8")
        nc.vector.tensor_reduce(out=cnt8[:], in_=ident[:].rearrange("p (n h) -> p n h", h=8), axis=AX.X, op=ALU.add)
        pool8 = const.tile([P, 16], BF16, name="pool8")
        nc.vector.tensor_scalar(out=pool8[:], in0=cnt8[:], scalar1=1.0 / 16.0, scalar2=None, op0=ALU.mult)
        cnt16 = const.tile([P, 8], F32, name="cnt16")
        nc.vector.tensor_reduce(out=cnt16[:], in_=ident[:].rearrange("p (n h) -> p n h", h=16), axis=AX.X, op=ALU.add)
        pool16 = const.tile([P, 8], BF16, name="pool16")
        nc.vector.tensor_scalar(out=pool16[:], in0=cnt16[:], scalar1=1.0 / 16.0, scalar2=None, op0=ALU.mult)

        kc = const.tile([P, NB], U32, name="kc", align_bytes=64)
        ks = const.tile([P, NB], U8, name="ks", align_bytes=64)
        weights = {}

        def fuel(target, count):
            wcodes, wscales = weights[("k", 0)]
            for j in range(count):
                nc.tensor.matmul_mx(out=target[:], lhsT=wcodes[:, 0:P].bitcast(FP8X4), lhsT_scale=wscales[:, 0:P], rhs=wcodes[:].bitcast(FP8X4), rhs_scale=wscales[:], start=True, stop=True)

        def st_sums(i):
            st = chunks[i]
            meanps = bank(0 if i % 2 == 0 else 7, [P, 2, P], F32, "meanps")
            st["mean"] = meanps
            x = st["x"]
            if st["wide"]:
                xv = x[:].rearrange("p (g d) -> p g d", g=16)
                for g in range(16):
                    for c in range(2):
                        nc.tensor.matmul(out=meanps[:, c, g * 8:(g + 1) * 8], lhsT=xv[:, g, c * P:(c + 1) * P], rhs=pool16[:], start=True, stop=True)
            else:
                xv = x[:].rearrange("p (g e) -> p g e", g=8)
                for g in range(8):
                    for c in range(2):
                        for l in range(2):
                            nc.tensor.matmul(out=meanps[:, c, g * 16:(g + 1) * 16], lhsT=xv[:, g, l * D + c * P:l * D + (c + 1) * P], rhs=pool8[:], start=(l == 0), stop=(l == 1))

        def st_l1(i):
            st = chunks[i]
            if st["wide"]:
                st["tsrc"] = st["x"][:].rearrange("p (g d) -> p g d", g=16)
                return
            xv = st["x"][:].rearrange("p (g e) -> p g e", g=8)
            l1 = work.tile([P, 8, D], BF16, name="l1", tag="l1")
            nc.vector.tensor_tensor(out=l1[:], in0=xv[:, :, 0:D], in1=xv[:, :, D:2 * D], op=ALU.max)
            st["tsrc"] = l1

        def st_transpose(i):
            st = chunks[i]
            halves = 2 if st["wide"] else 1
            perm = perm16 if st["wide"] else perm8
            src = st["tsrc"]
            st["tp"] = []
            for c in range(2):
                for half in range(halves):
                    j = c * halves + half
                    tp = bank(3 + j, [P, 8, P], BF16, "tp")
                    for g in range(8):
                        nc.tensor.transpose(out=tp[:, g, :], in_=src[:, half * 8 + g, c * P:(c + 1) * P], identity=perm[:])
                    hi = work.tile([P, 8, 64], BF16, name="hi", tag="hi%d" % j)
                    nc.scalar.copy(out=hi[:].rearrange("p g b -> p (g b)").bitcast(F32).rearrange("p (g b) -> p g b", g=8), in_=tp[:].rearrange("p g b -> p (g b)").bitcast(F32).rearrange("p (g b) -> p g b", g=8)[:, :, 32:64])
                    st["tp"].append((c, half, tp, hi))

        def st_tree(i):
            st = chunks[i]
            groups = 16 if st["wide"] else 8
            first = work.tile([P, 2, groups, 64], BF16, name="first", tag="first%d" % groups, bufs=2)
            for c, half, tp, hi in st["tp"]:
                nc.vector.tensor_tensor(out=first[:, c, half * 8:(half + 1) * 8, :], in0=tp[:, :, 0:64], in1=hi[:], op=ALU.max)
            cur = first
            width = 64
            while width > P // groups:
                width = width // 2
                nxt = work.tile([P, 2, groups, width], BF16, name="lvl", tag="lvl%d_%d" % (groups, width), bufs=2)
                nc.vector.tensor_tensor(out=nxt[:], in0=cur[:, :, :, 0:width], in1=cur[:, :, :, width:2 * width], op=ALU.max)
                cur = nxt
            grp = work.tile([P, P, 4], BF16, name="grp", tag="grp", align_bytes=64)
            nc.scalar.copy(out=grp[:, :, 0:2], in_=st["mean"][:].rearrange("p c b -> p b c"))
            nc.scalar.copy(out=grp[:, :, 2:4], in_=cur[:].rearrange("p c g b -> p (g b) c"))
            st["grp"] = grp

        def st_project(i):
            st = chunks[i]
            pc = work.tile([P, P], U32, name="pc", tag="pc", align_bytes=64)
            pscale = work.tile([P, P], U8, name="pscale", tag="pscale", align_bytes=64)
            nc.vector.quantize_mx(out=pc[:].bitcast(FP8X4), scales=pscale[:], in_=st["grp"][:].rearrange("p b t -> p (b t)"))
            wcodes, wscales = weights[(st["kind"], st["h"])]
            xps = bank(1, [P, HID], F32, "xps")
            fuel(xps, FUEL_P)
            nc.tensor.matmul_mx(out=xps[:], lhsT=pc[:].bitcast(FP8X4), lhsT_scale=pscale[:], rhs=wcodes[:].bitcast(FP8X4), rhs_scale=wscales[:], start=True, stop=True)
            st["xps"] = xps

        def st_rope(i):
            st = chunks[i]
            r = st["r"]
            xps = st["xps"]
            m1 = work.tile([P, HID], F32, name="m1", tag="m1")
            m2 = work.tile([P, HID], F32, name="m2", tag="m2")
            xc = work.tile([P, HID], F32, name="xc", tag="xc")
            nc.scalar.copy(out=xc[:], in_=xps[:])
            for half in range(2):
                hs = slice(half * 256, (half + 1) * 256)
                nc.gpsimd.tensor_tensor(out=m2[:, hs], in0=xc[:, hs], in1=tab[:, r, 1, hs], op=ALU.mult)
            nc.vector.tensor_tensor(out=m1[:], in0=xps[:], in1=tab[:, r, 0, :], op=ALU.mult)
            st["m"] = (m1, m2)

        def st_rope_turn(i):
            st = chunks[i]
            m1, m2 = st["m"]
            yt = bank(2, [P, 4, P], F32, "yt")
            for t in range(4):
                u = t ^ 2
                nc.tensor.matmul(out=yt[:, t, :], lhsT=m1[:, t * P:(t + 1) * P], rhs=identf[:], is_transpose=True, start=True, stop=False)
                nc.tensor.matmul(out=yt[:, t, :], lhsT=m2[:, u * P:(u + 1) * P], rhs=identf[:], is_transpose=True, start=False, stop=True)
            g2 = work.tile([P, P, 4], BF16, name="g2", tag="g2", align_bytes=64)
            nc.scalar.copy(out=g2[:], in_=yt[:].rearrange("p t b -> p b t"))
            st["g2"] = g2

        def st_scores(i):
            st = chunks[i]
            r = st["r"]
            g2v = st["g2"][:].rearrange("p b t -> p (b t)")
            if st["kind"] == "k":
                nc.vector.quantize_mx(out=kc[:, r * P:(r + 1) * P].bitcast(FP8X4), scales=ks[:, r * P:(r + 1) * P], in_=g2v)
                return
            qc = work.tile([P, P], U32, name="qc", tag="qc", align_bytes=64)
            qs = work.tile([P, P], U8, name="qs", tag="qs", align_bytes=64)
            nc.vector.quantize_mx(out=qc[:].bitcast(FP8X4), scales=qs[:], in_=g2v)
            st["sp"] = []
            for half in range(2):
                cols = slice(half * 512, (half + 1) * 512)
                sp = bank(5 + half, [P, 512], F32, "sp")
                if half == 0:
                    fuel(sp, FUEL_S)
                nc.tensor.matmul_mx(out=sp[:], lhsT=qc[:].bitcast(FP8X4), lhsT_scale=qs[:], rhs=kc[:, cols].bitcast(FP8X4), rhs_scale=ks[:, cols], start=True, stop=True)
                st["sp"].append(sp)

        def st_mask(r):
            bias = soft.tile([P, NB], BF16, name="bias", tag="bias", bufs=3)
            nc.scalar.activation(out=bias[:], in_=mask_tiles[r]["raw"][:].bitcast(U32).rearrange("p (w two) -> p w two", two=2)[:, :, 0], func=ACT.Copy, bias=-BIG, scale=BIG)
            mask_tiles[r]["bias"] = bias

        def st_softmax(i):
            st = chunks[i]
            bias = mask_tiles[st["r"]]["bias"]
            t_sb = soft.tile([P, NB], F32, name="t_sb", tag="t_sb")
            for half in range(2):
                cols = slice(half * 512, (half + 1) * 512)
                nc.vector.scalar_tensor_tensor(out=t_sb[:, cols], in0=st["sp"][half][:], scalar=SCALE, in1=bias[:, cols], op0=ALU.mult, op1=ALU.add)
            negm = soft.tile([P, 1], F32, name="negm", tag="negm")
            nc.vector.tensor_reduce(out=negm[:], in_=t_sb[:], axis=AX.X, op=ALU.max, negate=True)
            e_sb = soft.tile([P, NB], F32, name="e_sb", tag="e_sb")
            ssum = soft.tile([P, 1], F32, name="ssum", tag="ssum")
            nc.scalar.activation(out=e_sb[:], in_=t_sb[:], func=ACT.Exp, bias=negm[:], scale=1.0, accum_out=ssum[:])
            st["e"] = e_sb
            st["ssum"] = ssum

        def st_norm(i):
            st = chunks[i]
            rsum = soft.tile([P, 1], F32, name="rsum", tag="rsum")
            nc.vector.reciprocal(out=rsum[:], in_=st["ssum"][:])
            o_sb = soft.tile([P, NB], F32, name="o_sb", tag="o_sb", bufs=3)
            if i < n_chunks - 2:
                nc.scalar.activation(out=o_sb[:], in_=st["e"][:], func=ACT.Copy, scale=rsum[:])
            else:
                nc.vector.tensor_scalar(out=o_sb[:], in0=st["e"][:], scalar1=rsum[:], scalar2=None, op0=ALU.mult)
            st["o"] = o_sb

        def st_store(i):
            st = chunks[i]
            r = st["r"]
            nc.sync.dma_start(out=out[0, st["h"], r * P:(r + 1) * P, :], in_=st["o"][:])

        def is_q(i):
            return 0 <= i < n_chunks and chunks[i]["kind"] == "q"

        def valid(i):
            return 0 <= i < n_chunks

        raws = {}
        for n in range(n_chunks + 9):
            if is_q(n - 7):
                st_norm(n - 7)
            if is_q(n - 8):
                st_store(n - 8)
            if valid(n - 1):
                st_transpose(n - 1)
            if valid(n + PF):
                load_chunk(n + PF)
            if n == 2:
                raws[0] = load_weight(wq[0], "q0")
            if n == 3:
                raws[1] = load_weight(wq[1], "q1")
            if valid(n):
                st_sums(n)
            if n == 0:
                weights[("k", 0)] = prep_weight(raw_k, "k")
            if n == 5:
                weights[("q", 0)] = prep_weight(raws[0], "q0")
            if n == 6:
                weights[("q", 1)] = prep_weight(raws[1], "q1")
            if is_q(n - 2) and chunks[n - 2]["h"] == 0:
                st_mask(chunks[n - 2]["r"])
            if is_q(n - 6):
                st_softmax(n - 6)
            if valid(n - 4):
                st_rope_turn(n - 4)
            if valid(n - 3):
                st_rope(n - 3)
            if valid(n - 1):
                st_tree(n - 1)
            if n == 2:
                nc.vector.tensor_scalar(out=tab[:, :, 1, 256:512], in0=tab[:, :, 1, 256:512], scalar1=-1.0, scalar2=None, op0=ALU.mult)
            if valid(n - 2):
                st_project(n - 2)
            if valid(n - 5):
                st_scores(n - 5)
            if valid(n):
                st_l1(n)
